import numpy as np
import ml_dtypes


def mxq(x, axis, fmt="e4m3"):
    dtype, down = {"e4m3": (ml_dtypes.float8_e4m3fn, 7), "e5m2": (ml_dtypes.float8_e5m2, 14)}[fmt]
    v = np.moveaxis(np.asarray(x, np.float32).astype(ml_dtypes.bfloat16).astype(np.float64), axis, -1)
    blocks = v.reshape(v.shape[:-1] + (-1, 32))
    amax = np.abs(blocks).max(-1, keepdims=True)
    byte = np.maximum(np.where(amax > 0, np.frexp(amax)[1] - 1 + 127, 0) - down, 1)
    scale = np.exp2(byte - 127.0)
    codes = (blocks / scale).astype(np.float32).astype(dtype).astype(np.float64)
    return np.moveaxis((codes * scale).reshape(v.shape), -1, axis)


WIDE = False


def mx_kscale(k):
    if not WIDE:
        return np.ones(k)
    levels = np.array([10, -10, 5, -5, 0])
    a = np.random.permutation(np.resize(levels, k // 512 * 4)).reshape(k // 512, 4)
    idx = np.arange(k)
    return np.exp2(a[idx // 512, idx % 128 // 32])


BF16 = ml_dtypes.bfloat16


def bf(x):
    return np.asarray(x, np.float32).astype(BF16)


def f64(x):
    return np.asarray(x).astype(np.float64)


B, N, M, IN, R, MD = 2, 64, 4096, 128, 512, 128
G = 3 * R


def sigmoid(v):
    return 1.0 / (1.0 + np.exp(-v))


def setup_inputs():
    s = mx_kscale(R)
    u = s / s.max()
    return {"gi": bf(np.random.standard_normal((B, N, G)) * 0.9),
            "registers": bf(np.random.standard_normal((B, N, R)) * u),
            "W_hh": bf(np.random.standard_normal((G, R)) / np.sqrt(R) / u),
            "b_hh": bf(np.random.standard_normal(G) * 0.2),
            "W_out": bf(np.random.standard_normal((IN, R)) / np.sqrt(R)),
            "b_out": bf(np.random.standard_normal(IN) * 0.1)}


def reference(gi, registers, W_hh, b_hh, W_out, b_out):
    curr = f64(registers)
    gh = (mxq(curr, 2, "e4m3") @ mxq(f64(W_hh).T, 0, "e4m3")) + f64(b_hh)
    gi_r, gi_z, gi_n = np.split(f64(gi), 3, axis=-1)
    gh_r, gh_z, gh_n = np.split(gh, 3, axis=-1)
    r = sigmoid(gi_r + gh_r)
    z = sigmoid(gi_z + gh_z)
    n = np.tanh(gi_n + r * gh_n)
    new_regs = (1.0 - z) * n + z * curr
    output_active = (mxq(new_regs, 2, "e4m3") @ mxq(f64(W_out).T, 0, "e4m3")) + f64(b_out)
    return output_active, new_regs

@@ -1,0 +1,186 @@
+from contextlib import ExitStack
+
+import concourse.mybir as mybir
+from concourse.masks import make_identity
+
+F32 = mybir.dt.float32
+BF16 = mybir.dt.bfloat16
+U32 = mybir.dt.uint32
+U8 = mybir.dt.uint8
+FP8X4 = mybir.dt.float8_e4m3fn_x4
+ADD = mybir.AluOpType.add
+SUBTRACT = mybir.AluOpType.subtract
+MULT = mybir.AluOpType.mult
+SIGMOID = mybir.ActivationFunctionType.Sigmoid
+TANH = mybir.ActivationFunctionType.Tanh
+
+P = 128
+TOKENS = 128
+STATE = 512
+OUT = 128
+PACK = 4
+GATES = 3
+GATE_R, GATE_Z, GATE_N = 0, 1, 2
+OLD_STATE = 3
+UNITS = 2
+ROWS = 2
+
+FLOPS = 2 * TOKENS * STATE * (GATES * STATE + OUT)
+
+
+def tile_vectorizednpu_pb_s_kernel(tc, gi, registers, W_hh, b_hh, W_out, b_out, out_0, out_1):
+    nc = tc.nc
+    with ExitStack() as ctx:
+        keep = ctx.enter_context(tc.tile_pool(name="keep", bufs=1))
+        per_unit = ctx.enter_context(tc.tile_pool(name="per_unit", bufs=GATES * UNITS))
+        flipped = ctx.enter_context(tc.psum_pool(name="flipped", bufs=4))
+        products = ctx.enter_context(tc.psum_pool(name="products", bufs=3))
+
+        regs_in = keep.tile([TOKENS, STATE], BF16)
+        nc.sync.dma_start(out=regs_in[:], in_=registers.flatten_outer_dims())
+        w_view = W_hh.rearrange("(g p u e) k -> g u p e k", g=GATES, p=P, u=UNITS, e=ROWS)
+        w_rows = {}
+
+        def load_weights(g):
+            for u in range(UNITS):
+                w_rows[(g, u)] = per_unit.tile([P, ROWS, STATE], BF16, name="w_rows")
+                nc.sync.dma_start(out=w_rows[(g, u)][:], in_=w_view[g, u])
+
+        load_weights(GATE_R)
+        gi_in = keep.tile([TOKENS, GATES * STATE], BF16)
+        nc.sync.dma_start(out=gi_in[:], in_=gi.flatten_outer_dims())
+        load_weights(GATE_N)
+        load_weights(GATE_Z)
+        wout_in = keep.tile([OUT, STATE], BF16)
+        nc.sync.dma_start(out=wout_in[:], in_=W_out)
+        bout_all = keep.tile([P, OUT], BF16)
+        nc.sync.dma_start(out=bout_all[:], in_=b_out.partition_broadcast(P))
+        bias_in = keep.tile([P, GATES, PACK], BF16)
+        nc.scalar.dma_start(out=bias_in[:], in_=b_hh.rearrange("(g p j) -> p g j", g=GATES, j=PACK))
+
+        identity = keep.tile([P, P], F32)
+        make_identity(nc, identity[:])
+        warm = keep.tile([P, 1], F32)
+        nc.vector.memset(warm[:], 0.0)
+        nc.scalar.activation(out=warm[:], in_=warm[:], func=SIGMOID)
+        bias = keep.tile([P, GATES, PACK], F32)
+        nc.vector.tensor_copy(out=bias[:], in_=bias_in[:])
+
+        def quantise(grouped, width, name):
+            codes = per_unit.tile([P, width], U32, align_bytes=64, name=name + "_codes")
+            scales = per_unit.tile([P, width], U8, align_bytes=64, name=name + "_scales")
+            nc.vector.quantize_mx(out=codes[:].bitcast(FP8X4), scales=scales[:], in_=grouped)
+            return codes, scales
+
+        reg_words = regs_in[:].bitcast(F32)
+        reg_bank = flipped.tile([P, 4, P], F32, tag="bank")
+        for v in range(2):
+            nc.tensor.transpose(out=reg_bank[:, v, :], in_=reg_words[:, v * P : (v + 1) * P], identity=identity[:])
+        reg_grouped = keep.tile([P, TOKENS, PACK], BF16, align_bytes=64)
+        nc.scalar.copy(out=reg_grouped[:].bitcast(F32), in_=reg_bank[:, 0:2, :].rearrange("q v t -> q t v"))
+        reg_codes, reg_scales = quantise(reg_grouped[:].rearrange("q t k -> q (t k)"), TOKENS, "reg")
+
+        gi_words = gi_in[:].bitcast(F32).rearrange("t (g p u) -> t g u p", g=GATES, u=UNITS)
+        token_major = [gi_words[:, g] for g in range(GATES)] + [reg_words.rearrange("t (p u) -> t u p", u=UNITS)]
+        side = keep.tile([P, 4, UNITS, TOKENS], F32)
+        for half in range(2):
+            side_bank = flipped.tile([P, 4, P], F32, tag="bank")
+            for i in range(2):
+                for u in range(UNITS):
+                    nc.tensor.transpose(
+                        out=side_bank[:, 2 * i + u, :], in_=token_major[2 * half + i][:, u, :], identity=identity[:]
+                    )
+            nc.scalar.copy(
+                out=side[:, 2 * half : 2 * half + 2].rearrange("p b u t -> p (b u) t"), in_=side_bank[:]
+            )
+        side_values = side[:].bitcast(BF16).rearrange("p b u (t e) -> p b u e t", e=ROWS)
+
+        def hidden_product(g, u):
+            words = w_rows[(g, u)][:].bitcast(F32)
+            w_bank = flipped.tile([P, 4, P], F32, tag="bank")
+            for e in range(ROWS):
+                for v in range(2):
+                    nc.tensor.transpose(
+                        out=w_bank[:, 2 * e + v, :], in_=words[:, e, v * P : (v + 1) * P], identity=identity[:]
+                    )
+            w_grouped = per_unit.tile([P, ROWS, P, PACK], BF16, align_bytes=64)
+            nc.scalar.copy(out=w_grouped[:].bitcast(F32), in_=w_bank[:].rearrange("q (e v) m -> q e m v", v=2))
+            w_codes, w_scales = quantise(w_grouped[:].rearrange("q e m k -> q (e m k)"), ROWS * P, "w")
+            gh = products.tile([P, ROWS, TOKENS], F32, tag="product")
+            for e in range(ROWS):
+                nc.tensor.matmul_mx(
+                    out=gh[:, e, :],
+                    lhsT=w_codes[:, e * P : (e + 1) * P].bitcast(FP8X4),
+                    lhsT_scale=w_scales[:, e * P : (e + 1) * P],
+                    rhs=reg_codes[:].bitcast(FP8X4),
+                    rhs_scale=reg_scales[:],
+                    start=True,
+                    stop=True,
+                )
+            return gh
+
+        def add_bias_then(op, g, u, gh, other, name):
+            result = per_unit.tile([P, ROWS, TOKENS], F32, name=name)
+            for e in range(ROWS):
+                j = ROWS * u + e
+                nc.vector.scalar_tensor_tensor(
+                    out=result[:, e, :], in0=gh[:, e, :], scalar=bias[:, g, j : j + 1], in1=other[:, e, :], op0=ADD, op1=op
+                )
+            return result
+
+        reset = keep.tile([P, UNITS, ROWS, TOKENS], F32)
+        candidate = keep.tile([P, UNITS, ROWS, TOKENS], F32)
+        gap = keep.tile([P, UNITS, ROWS, TOKENS], F32)
+        new_state = keep.tile([P, UNITS, ROWS, TOKENS], F32)
+
+        for u in range(UNITS):
+            gh = hidden_product(GATE_R, u)
+            r_arg = add_bias_then(ADD, GATE_R, u, gh, side_values[:, GATE_R, u], "r_arg")
+            nc.scalar.activation(out=reset[:, u], in_=r_arg[:], func=SIGMOID)
+
+        for u in range(UNITS):
+            gh = hidden_product(GATE_N, u)
+            n_arg = add_bias_then(MULT, GATE_N, u, gh, reset[:, u], "n_arg")
+            nc.vector.tensor_tensor(out=n_arg[:], in0=n_arg[:], in1=side_values[:, GATE_N, u], op=ADD)
+            nc.scalar.activation(out=candidate[:, u], in_=n_arg[:], func=TANH)
+            nc.vector.tensor_tensor(out=gap[:, u], in0=side_values[:, OLD_STATE, u], in1=candidate[:, u], op=SUBTRACT)
+
+        wout_words = wout_in[:].bitcast(F32).rearrange("o (p u) -> o u p", u=UNITS)
+        wout_bank = flipped.tile([P, 4, P], F32, tag="bank")
+        for u in range(UNITS):
+            nc.tensor.transpose(out=wout_bank[:, u, :], in_=wout_words[:, u, :], identity=identity[:])
+        wout_grouped = keep.tile([P, OUT, PACK], BF16, align_bytes=64)
+        nc.scalar.copy(out=wout_grouped[:].bitcast(F32), in_=wout_bank[:, 0:2, :].rearrange("p u o -> p o u"))
+        wout_codes, wout_scales = quantise(wout_grouped[:].rearrange("p o k -> p (o k)"), OUT, "wout")
+
+        for u in range(UNITS):
+            gh = hidden_product(GATE_Z, u)
+            z_arg = add_bias_then(ADD, GATE_Z, u, gh, side_values[:, GATE_Z, u], "z_arg")
+            nc.scalar.activation(out=z_arg[:], in_=z_arg[:], func=SIGMOID)
+            nc.vector.tensor_tensor(out=z_arg[:], in0=z_arg[:], in1=gap[:, u], op=MULT)
+            nc.vector.tensor_tensor(out=new_state[:, u], in0=z_arg[:], in1=candidate[:, u], op=ADD)
+
+        new_by_j = new_state[:].rearrange("p u e t -> p (u e) t")
+        new_grouped = keep.tile([P, TOKENS, PACK], BF16, align_bytes=64)
+        nc.vector.tensor_copy(out=new_grouped[:], in_=new_by_j.rearrange("p j t -> p t j"))
+        new_codes, new_scales = quantise(new_grouped[:].rearrange("p t k -> p (t k)"), TOKENS, "new")
+        active = products.tile([TOKENS, OUT], F32, tag="product")
+        nc.tensor.matmul_mx(
+            out=active[:],
+            lhsT=new_codes[:].bitcast(FP8X4),
+            lhsT_scale=new_scales[:],
+            rhs=wout_codes[:].bitcast(FP8X4),
+            rhs_scale=wout_scales[:],
+            start=True,
+            stop=True,
+        )
+        active_out = keep.tile([TOKENS, OUT], F32)
+        nc.vector.tensor_tensor(out=active_out[:], in0=active[:], in1=bout_all[:], op=ADD)
+        nc.sync.dma_start(out=out_0.flatten_outer_dims(), in_=active_out[:])
+
+        back_bank = flipped.tile([TOKENS, PACK, P], F32, tag="bank")
+        for j in range(PACK):
+            nc.tensor.transpose(out=back_bank[:, j, :], in_=new_by_j[:, j, :], identity=identity[:])
+        new_out = keep.tile([TOKENS, P, PACK], F32)
+        nc.scalar.copy(out=new_out[:], in_=back_bank[:].rearrange("t j p -> t p j"))
+        nc.sync.dma_start(out=out_1.flatten_outer_dims(), in_=new_out[:].rearrange("t p j -> t (p j)"))

@@ -18,12 +18,13 @@ P = 128
 TOKENS = 128
 STATE = 512
 OUT = 128
-PACK = 4
+HALVES = 2
+PAIR = 2
+PACK = HALVES * PAIR
 GATES = 3
 GATE_R, GATE_Z, GATE_N = 0, 1, 2
-OLD_STATE = 3
-UNITS = 2
-ROWS = 2
+GATE_ORDER = (GATE_R, GATE_N, GATE_Z)
+BANK_SLOTS = 4
 
 FLOPS = 2 * TOKENS * STATE * (GATES * STATE + OUT)
 
@@ -32,39 +33,45 @@ def tile_vectorizednpu_pb_s_kernel(tc, gi, registers, W_hh, b_hh, W_out, b_out, 
     nc = tc.nc
     with ExitStack() as ctx:
         keep = ctx.enter_context(tc.tile_pool(name="keep", bufs=1))
-        per_unit = ctx.enter_context(tc.tile_pool(name="per_unit", bufs=GATES * UNITS))
-        flipped = ctx.enter_context(tc.psum_pool(name="flipped", bufs=4))
+        per_unit = ctx.enter_context(tc.tile_pool(name="per_unit", bufs=GATES * HALVES))
+        flipped = ctx.enter_context(tc.psum_pool(name="flipped", bufs=5))
         products = ctx.enter_context(tc.psum_pool(name="products", bufs=3))
 
         regs_in = keep.tile([TOKENS, STATE], BF16)
         nc.sync.dma_start(out=regs_in[:], in_=registers.flatten_outer_dims())
-        w_view = W_hh.rearrange("(g p u e) k -> g u p e k", g=GATES, p=P, u=UNITS, e=ROWS)
+        bias_rows = keep.tile([P, HALVES * P], BF16)
+        nc.vector.memset(bias_rows[:], 0.0)
+        nc.sync.dma_start(out=bias_rows[0 : GATES * HALVES, :], in_=b_hh.rearrange("(r c) -> r c", c=HALVES * P))
+        w_view = W_hh.rearrange("(g v p e) k -> g v p e k", g=GATES, v=HALVES, p=P, e=PAIR)
+        gi_flat = gi.flatten_outer_dims()
+        gi_in = {}
         w_rows = {}
-
-        def load_weights(g):
-            for u in range(UNITS):
-                w_rows[(g, u)] = per_unit.tile([P, ROWS, STATE], BF16, name="w_rows")
-                nc.sync.dma_start(out=w_rows[(g, u)][:], in_=w_view[g, u])
-
-        load_weights(GATE_R)
-        gi_in = keep.tile([TOKENS, GATES * STATE], BF16)
-        nc.sync.dma_start(out=gi_in[:], in_=gi.flatten_outer_dims())
-        load_weights(GATE_N)
-        load_weights(GATE_Z)
+        for g in GATE_ORDER:
+            for v in range(HALVES):
+                w_rows[(g, v)] = per_unit.tile([P, PAIR, STATE], BF16, name="w_rows")
+                nc.sync.dma_start(out=w_rows[(g, v)][:], in_=w_view[g, v])
+            gi_in[g] = keep.tile([TOKENS, STATE], BF16, name="gi_in%d" % g)
+            nc.sync.dma_start(out=gi_in[g][:], in_=gi_flat[:, g * STATE : (g + 1) * STATE])
         wout_in = keep.tile([OUT, STATE], BF16)
         nc.sync.dma_start(out=wout_in[:], in_=W_out)
         bout_all = keep.tile([P, OUT], BF16)
         nc.sync.dma_start(out=bout_all[:], in_=b_out.partition_broadcast(P))
-        bias_in = keep.tile([P, GATES, PACK], BF16)
-        nc.scalar.dma_start(out=bias_in[:], in_=b_hh.rearrange("(g p j) -> p g j", g=GATES, j=PACK))
 
         identity = keep.tile([P, P], F32)
         make_identity(nc, identity[:])
         warm = keep.tile([P, 1], F32)
         nc.vector.memset(warm[:], 0.0)
         nc.scalar.activation(out=warm[:], in_=warm[:], func=SIGMOID)
-        bias = keep.tile([P, GATES, PACK], F32)
-        nc.vector.tensor_copy(out=bias[:], in_=bias_in[:])
+
+        def flip(bank, slot, words):
+            nc.tensor.transpose(out=bank[:, slot, :], in_=words, identity=identity[:])
+
+        def flip_rows(rows_in):
+            words = rows_in[:].bitcast(F32)
+            bank = flipped.tile([P, BANK_SLOTS, P], F32, tag="bank")
+            for v in range(HALVES):
+                flip(bank, v, words[:, v * P : (v + 1) * P])
+            return bank[:, 0:HALVES, :]
 
         def quantise(grouped, width, name):
             codes = per_unit.tile([P, width], U32, align_bytes=64, name=name + "_codes")
@@ -72,115 +79,111 @@ def tile_vectorizednpu_pb_s_kernel(tc, gi, registers, W_hh, b_hh, W_out, b_out, 
             nc.vector.quantize_mx(out=codes[:].bitcast(FP8X4), scales=scales[:], in_=grouped)
             return codes, scales
 
-        reg_words = regs_in[:].bitcast(F32)
-        reg_bank = flipped.tile([P, 4, P], F32, tag="bank")
-        for v in range(2):
-            nc.tensor.transpose(out=reg_bank[:, v, :], in_=reg_words[:, v * P : (v + 1) * P], identity=identity[:])
-        reg_grouped = keep.tile([P, TOKENS, PACK], BF16, align_bytes=64)
-        nc.scalar.copy(out=reg_grouped[:].bitcast(F32), in_=reg_bank[:, 0:2, :].rearrange("q v t -> q t v"))
-        reg_codes, reg_scales = quantise(reg_grouped[:].rearrange("q t k -> q (t k)"), TOKENS, "reg")
+        def rows_to_operand(rows_in, name):
+            grouped = keep.tile([P, P, PACK], BF16, align_bytes=64, name=name + "_grouped")
+            nc.scalar.copy(out=grouped[:].bitcast(F32), in_=flip_rows(rows_in).rearrange("p v m -> p m v"))
+            return grouped, quantise(grouped[:].rearrange("p m k -> p (m k)"), P, name)
 
-        gi_words = gi_in[:].bitcast(F32).rearrange("t (g p u) -> t g u p", g=GATES, u=UNITS)
-        token_major = [gi_words[:, g] for g in range(GATES)] + [reg_words.rearrange("t (p u) -> t u p", u=UNITS)]
-        side = keep.tile([P, 4, UNITS, TOKENS], F32)
-        for half in range(2):
-            side_bank = flipped.tile([P, 4, P], F32, tag="bank")
-            for i in range(2):
-                for u in range(UNITS):
-                    nc.tensor.transpose(
-                        out=side_bank[:, 2 * i + u, :], in_=token_major[2 * half + i][:, u, :], identity=identity[:]
-                    )
-            nc.scalar.copy(
-                out=side[:, 2 * half : 2 * half + 2].rearrange("p b u t -> p (b u) t"), in_=side_bank[:]
+        def multiply(out, stationary, moving):
+            nc.tensor.matmul_mx(
+                out=out,
+                lhsT=stationary[0].bitcast(FP8X4),
+                lhsT_scale=stationary[1],
+                rhs=moving[0][:].bitcast(FP8X4),
+                rhs_scale=moving[1][:],
+                start=True,
+                stop=True,
             )
-        side_values = side[:].bitcast(BF16).rearrange("p b u (t e) -> p b u e t", e=ROWS)
 
-        def hidden_product(g, u):
-            words = w_rows[(g, u)][:].bitcast(F32)
-            w_bank = flipped.tile([P, 4, P], F32, tag="bank")
-            for e in range(ROWS):
-                for v in range(2):
-                    nc.tensor.transpose(
-                        out=w_bank[:, 2 * e + v, :], in_=words[:, e, v * P : (v + 1) * P], identity=identity[:]
-                    )
-            w_grouped = per_unit.tile([P, ROWS, P, PACK], BF16, align_bytes=64)
-            nc.scalar.copy(out=w_grouped[:].bitcast(F32), in_=w_bank[:].rearrange("q (e v) m -> q e m v", v=2))
-            w_codes, w_scales = quantise(w_grouped[:].rearrange("q e m k -> q (e m k)"), ROWS * P, "w")
-            gh = products.tile([P, ROWS, TOKENS], F32, tag="product")
-            for e in range(ROWS):
-                nc.tensor.matmul_mx(
-                    out=gh[:, e, :],
-                    lhsT=w_codes[:, e * P : (e + 1) * P].bitcast(FP8X4),
-                    lhsT_scale=w_scales[:, e * P : (e + 1) * P],
-                    rhs=reg_codes[:].bitcast(FP8X4),
-                    rhs_scale=reg_scales[:],
-                    start=True,
-                    stop=True,
-                )
+        reg_grouped, reg_operand = rows_to_operand(regs_in, "reg")
+        old_state = reg_grouped[:].rearrange("p t (v e) -> p v e t", e=PAIR)
+        bias_bank = flipped.tile([P, BANK_SLOTS, P], F32, tag="bank")
+        flip(bias_bank, 0, bias_rows[:].bitcast(F32))
+        bias = keep.tile([P, GATES * HALVES, PAIR], F32)
+        nc.vector.tensor_copy(
+            out=bias[:].rearrange("p r e -> p (r e)"), in_=bias_bank[:, 0, 0 : GATES * HALVES].bitcast(BF16)
+        )
+
+        def hidden_product(g, v):
+            words = w_rows[(g, v)][:].bitcast(F32)
+            bank = flipped.tile([P, BANK_SLOTS, P], F32, tag="bank")
+            for e in range(PAIR):
+                for k_half in range(HALVES):
+                    flip(bank, HALVES * e + k_half, words[:, e, k_half * P : (k_half + 1) * P])
+            w_grouped = per_unit.tile([P, PAIR, P, PACK], BF16, align_bytes=64)
+            nc.scalar.copy(out=w_grouped[:].bitcast(F32), in_=bank[:].rearrange("p (e h) m -> p e m h", h=HALVES))
+            w_codes, w_scales = quantise(w_grouped[:].rearrange("p e m k -> p (e m k)"), PAIR * P, "w")
+            gh = products.tile([P, PAIR, TOKENS], F32, tag="product")
+            for e in range(PAIR):
+                rows = slice(e * P, (e + 1) * P)
+                multiply(gh[:, e, :], (w_codes[:, rows], w_scales[:, rows]), reg_operand)
             return gh
 
-        def add_bias_then(op, g, u, gh, other, name):
-            result = per_unit.tile([P, ROWS, TOKENS], F32, name=name)
-            for e in range(ROWS):
-                j = ROWS * u + e
+        def gi_of_gate(g):
+            gi_words = keep.tile([P, HALVES, TOKENS], F32, name="gi_words%d" % g)
+            nc.scalar.copy(out=gi_words[:], in_=flip_rows(gi_in[g]))
+            return gi_words[:].bitcast(BF16).rearrange("p v (t e) -> p v e t", e=PAIR)
+
+        def add_bias_then(op, g, v, gh, other):
+            result = per_unit.tile([P, PAIR, TOKENS], F32, name="arg")
+            for e in range(PAIR):
                 nc.vector.scalar_tensor_tensor(
-                    out=result[:, e, :], in0=gh[:, e, :], scalar=bias[:, g, j : j + 1], in1=other[:, e, :], op0=ADD, op1=op
+                    out=result[:, e, :],
+                    in0=gh[:, e, :],
+                    scalar=bias[:, HALVES * g + v, e : e + 1],
+                    in1=other[:, e, :],
+                    op0=ADD,
+                    op1=op,
                 )
             return result
 
-        reset = keep.tile([P, UNITS, ROWS, TOKENS], F32)
-        candidate = keep.tile([P, UNITS, ROWS, TOKENS], F32)
-        gap = keep.tile([P, UNITS, ROWS, TOKENS], F32)
-        new_state = keep.tile([P, UNITS, ROWS, TOKENS], F32)
-
-        for u in range(UNITS):
-            gh = hidden_product(GATE_R, u)
-            r_arg = add_bias_then(ADD, GATE_R, u, gh, side_values[:, GATE_R, u], "r_arg")
-            nc.scalar.activation(out=reset[:, u], in_=r_arg[:], func=SIGMOID)
-
-        for u in range(UNITS):
-            gh = hidden_product(GATE_N, u)
-            n_arg = add_bias_then(MULT, GATE_N, u, gh, reset[:, u], "n_arg")
-            nc.vector.tensor_tensor(out=n_arg[:], in0=n_arg[:], in1=side_values[:, GATE_N, u], op=ADD)
-            nc.scalar.activation(out=candidate[:, u], in_=n_arg[:], func=TANH)
-            nc.vector.tensor_tensor(out=gap[:, u], in0=side_values[:, OLD_STATE, u], in1=candidate[:, u], op=SUBTRACT)
-
-        wout_words = wout_in[:].bitcast(F32).rearrange("o (p u) -> o u p", u=UNITS)
-        wout_bank = flipped.tile([P, 4, P], F32, tag="bank")
-        for u in range(UNITS):
-            nc.tensor.transpose(out=wout_bank[:, u, :], in_=wout_words[:, u, :], identity=identity[:])
-        wout_grouped = keep.tile([P, OUT, PACK], BF16, align_bytes=64)
-        nc.scalar.copy(out=wout_grouped[:].bitcast(F32), in_=wout_bank[:, 0:2, :].rearrange("p u o -> p o u"))
-        wout_codes, wout_scales = quantise(wout_grouped[:].rearrange("p o k -> p (o k)"), OUT, "wout")
-
-        for u in range(UNITS):
-            gh = hidden_product(GATE_Z, u)
-            z_arg = add_bias_then(ADD, GATE_Z, u, gh, side_values[:, GATE_Z, u], "z_arg")
-            nc.scalar.activation(out=z_arg[:], in_=z_arg[:], func=SIGMOID)
-            nc.vector.tensor_tensor(out=z_arg[:], in0=z_arg[:], in1=gap[:, u], op=MULT)
-            nc.vector.tensor_tensor(out=new_state[:, u], in0=z_arg[:], in1=candidate[:, u], op=ADD)
-
-        new_by_j = new_state[:].rearrange("p u e t -> p (u e) t")
+        reset = keep.tile([P, HALVES, PAIR, TOKENS], F32)
+        candidate = keep.tile([P, HALVES, PAIR, TOKENS], F32)
+        gap = keep.tile([P, HALVES, PAIR, TOKENS], F32)
+        new_state = keep.tile([P, HALVES, PAIR, TOKENS], F32)
         new_grouped = keep.tile([P, TOKENS, PACK], BF16, align_bytes=64)
-        nc.vector.tensor_copy(out=new_grouped[:], in_=new_by_j.rearrange("p j t -> p t j"))
+        out_1_flat = out_1.flatten_outer_dims()
+
+        products_r = [hidden_product(GATE_R, v) for v in range(HALVES)]
+        gi_r = gi_of_gate(GATE_R)
+        for v in range(HALVES):
+            arg = add_bias_then(ADD, GATE_R, v, products_r[v], gi_r[:, v])
+            nc.scalar.activation(out=reset[:, v], in_=arg[:], func=SIGMOID)
+
+        products_n = [hidden_product(GATE_N, v) for v in range(HALVES)]
+        gi_n = gi_of_gate(GATE_N)
+        for v in range(HALVES):
+            arg = add_bias_then(MULT, GATE_N, v, products_n[v], reset[:, v])
+            nc.vector.tensor_tensor(out=arg[:], in0=arg[:], in1=gi_n[:, v], op=ADD)
+            nc.scalar.activation(out=candidate[:, v], in_=arg[:], func=TANH)
+            nc.vector.tensor_tensor(out=gap[:, v], in0=old_state[:, v], in1=candidate[:, v], op=SUBTRACT)
+
+        products_z = [hidden_product(GATE_Z, v) for v in range(HALVES)]
+        gi_z = gi_of_gate(GATE_Z)
+        for v in range(HALVES):
+            arg = add_bias_then(ADD, GATE_Z, v, products_z[v], gi_z[:, v])
+            nc.scalar.activation(out=arg[:], in_=arg[:], func=SIGMOID)
+            nc.vector.tensor_tensor(out=arg[:], in0=arg[:], in1=gap[:, v], op=MULT)
+            nc.vector.tensor_tensor(out=new_state[:, v], in0=arg[:], in1=candidate[:, v], op=ADD)
+            nc.scalar.copy(
+                out=new_grouped[:].rearrange("p t (v e) -> p v t e", e=PAIR)[:, v],
+                in_=new_state[:, v].rearrange("p e t -> p t e"),
+            )
+
+        wout_grouped, wout_operand = rows_to_operand(wout_in, "wout")
         new_codes, new_scales = quantise(new_grouped[:].rearrange("p t k -> p (t k)"), TOKENS, "new")
         active = products.tile([TOKENS, OUT], F32, tag="product")
-        nc.tensor.matmul_mx(
-            out=active[:],
-            lhsT=new_codes[:].bitcast(FP8X4),
-            lhsT_scale=new_scales[:],
-            rhs=wout_codes[:].bitcast(FP8X4),
-            rhs_scale=wout_scales[:],
-            start=True,
-            stop=True,
-        )
+        multiply(active[:], (new_codes[:], new_scales[:]), wout_operand)
         active_out = keep.tile([TOKENS, OUT], F32)
         nc.vector.tensor_tensor(out=active_out[:], in0=active[:], in1=bout_all[:], op=ADD)
         nc.sync.dma_start(out=out_0.flatten_outer_dims(), in_=active_out[:])
 
-        back_bank = flipped.tile([TOKENS, PACK, P], F32, tag="bank")
-        for j in range(PACK):
-            nc.tensor.transpose(out=back_bank[:, j, :], in_=new_by_j[:, j, :], identity=identity[:])
-        new_out = keep.tile([TOKENS, P, PACK], F32)
-        nc.scalar.copy(out=new_out[:], in_=back_bank[:].rearrange("t j p -> t p j"))
-        nc.sync.dma_start(out=out_1.flatten_outer_dims(), in_=new_out[:].rearrange("t p j -> t (p j)"))
+        for v in range(HALVES):
+            back = flipped.tile([TOKENS, BANK_SLOTS, P], F32, tag="bank")
+            for e in range(PAIR):
+                flip(back, e, new_state[:, v, e, :])
+            new_out = per_unit.tile([TOKENS, P, PAIR], F32, name="new_out")
+            nc.scalar.copy(out=new_out[:], in_=back[:, 0:PAIR, :].rearrange("t e p -> t p e"))
+            nc.sync.dma_start(
+                out=out_1_flat[:, v * PAIR * P : (v + 1) * PAIR * P], in_=new_out[:].rearrange("t p e -> t (p e)")
+            )

@@ -31,7 +31,9 @@ FLOPS = 2 * TOKENS * STATE * (GATES * STATE + OUT)
 
 def tile_vectorizednpu_pb_s_kernel(tc, gi, registers, W_hh, b_hh, W_out, b_out, out_0, out_1):
     nc = tc.nc
+    units = [(g, v) for g in GATE_ORDER for v in range(HALVES)]
     with ExitStack() as ctx:
+        ctx.enter_context(tc.manual_schedule())
         keep = ctx.enter_context(tc.tile_pool(name="keep", bufs=1))
         per_unit = ctx.enter_context(tc.tile_pool(name="per_unit", bufs=GATES * HALVES))
         flipped = ctx.enter_context(tc.psum_pool(name="flipped", bufs=5))
@@ -79,10 +81,10 @@ def tile_vectorizednpu_pb_s_kernel(tc, gi, registers, W_hh, b_hh, W_out, b_out, 
             nc.vector.quantize_mx(out=codes[:].bitcast(FP8X4), scales=scales[:], in_=grouped)
             return codes, scales
 
-        def rows_to_operand(rows_in, name):
+        def regrouped(rows_in, name):
             grouped = keep.tile([P, P, PACK], BF16, align_bytes=64, name=name + "_grouped")
             nc.scalar.copy(out=grouped[:].bitcast(F32), in_=flip_rows(rows_in).rearrange("p v m -> p m v"))
-            return grouped, quantise(grouped[:].rearrange("p m k -> p (m k)"), P, name)
+            return grouped
 
         def multiply(out, stationary, moving):
             nc.tensor.matmul_mx(
@@ -95,7 +97,7 @@ def tile_vectorizednpu_pb_s_kernel(tc, gi, registers, W_hh, b_hh, W_out, b_out, 
                 stop=True,
             )
 
-        reg_grouped, reg_operand = rows_to_operand(regs_in, "reg")
+        reg_grouped = regrouped(regs_in, "reg")
         old_state = reg_grouped[:].rearrange("p t (v e) -> p v e t", e=PAIR)
         bias_bank = flipped.tile([P, BANK_SLOTS, P], F32, tag="bank")
         flip(bias_bank, 0, bias_rows[:].bitcast(F32))
@@ -103,87 +105,110 @@ def tile_vectorizednpu_pb_s_kernel(tc, gi, registers, W_hh, b_hh, W_out, b_out, 
         nc.vector.tensor_copy(
             out=bias[:].rearrange("p r e -> p (r e)"), in_=bias_bank[:, 0, 0 : GATES * HALVES].bitcast(BF16)
         )
+        reg_operand = quantise(reg_grouped[:].rearrange("p m k -> p (m k)"), TOKENS, "reg")
 
-        def hidden_product(g, v):
-            words = w_rows[(g, v)][:].bitcast(F32)
+        gi_values = {}
+        w_grouped = {}
+        w_operand = {}
+        gate_arg = {}
+        back = {}
+        reset = keep.tile([P, HALVES, PAIR, TOKENS], F32)
+        candidate = keep.tile([P, HALVES, PAIR, TOKENS], F32)
+        update = keep.tile([P, HALVES, PAIR, TOKENS], F32)
+        gate_value = {GATE_R: reset, GATE_N: candidate, GATE_Z: update}
+        gap = keep.tile([P, HALVES, PAIR, TOKENS], F32)
+        new_state = keep.tile([P, HALVES, PAIR, TOKENS], F32)
+        new_grouped = keep.tile([P, TOKENS, PACK], BF16, align_bytes=64)
+
+        def flip_weights(i):
+            words = w_rows[units[i]][:].bitcast(F32)
             bank = flipped.tile([P, BANK_SLOTS, P], F32, tag="bank")
             for e in range(PAIR):
                 for k_half in range(HALVES):
                     flip(bank, HALVES * e + k_half, words[:, e, k_half * P : (k_half + 1) * P])
-            w_grouped = per_unit.tile([P, PAIR, P, PACK], BF16, align_bytes=64)
-            nc.scalar.copy(out=w_grouped[:].bitcast(F32), in_=bank[:].rearrange("p (e h) m -> p e m h", h=HALVES))
-            w_codes, w_scales = quantise(w_grouped[:].rearrange("p e m k -> p (e m k)"), PAIR * P, "w")
+            w_grouped[i] = per_unit.tile([P, PAIR, P, PACK], BF16, align_bytes=64, name="w_grouped")
+            nc.scalar.copy(out=w_grouped[i][:].bitcast(F32), in_=bank[:].rearrange("p (e h) m -> p e m h", h=HALVES))
+
+        def quantise_weights(i):
+            w_operand[i] = quantise(w_grouped[i][:].rearrange("p e m k -> p (e m k)"), PAIR * P, "w")
+
+        def gate_argument(i):
+            g, v = units[i]
+            w_codes, w_scales = w_operand[i]
             gh = products.tile([P, PAIR, TOKENS], F32, tag="product")
             for e in range(PAIR):
                 rows = slice(e * P, (e + 1) * P)
                 multiply(gh[:, e, :], (w_codes[:, rows], w_scales[:, rows]), reg_operand)
-            return gh
-
-        def gi_of_gate(g):
-            gi_words = keep.tile([P, HALVES, TOKENS], F32, name="gi_words%d" % g)
-            nc.scalar.copy(out=gi_words[:], in_=flip_rows(gi_in[g]))
-            return gi_words[:].bitcast(BF16).rearrange("p v (t e) -> p v e t", e=PAIR)
-
-        def add_bias_then(op, g, v, gh, other):
-            result = per_unit.tile([P, PAIR, TOKENS], F32, name="arg")
+            other, op = (reset[:, v], MULT) if g == GATE_N else (gi_values[g][:, v], ADD)
+            gate_arg[i] = per_unit.tile([P, PAIR, TOKENS], F32, name="gate_arg")
             for e in range(PAIR):
                 nc.vector.scalar_tensor_tensor(
-                    out=result[:, e, :],
+                    out=gate_arg[i][:, e, :],
                     in0=gh[:, e, :],
                     scalar=bias[:, HALVES * g + v, e : e + 1],
                     in1=other[:, e, :],
                     op0=ADD,
                     op1=op,
                 )
-            return result
+            if g == GATE_N:
+                nc.vector.tensor_tensor(out=gate_arg[i][:], in0=gate_arg[i][:], in1=gi_values[g][:, v], op=ADD)
 
-        reset = keep.tile([P, HALVES, PAIR, TOKENS], F32)
-        candidate = keep.tile([P, HALVES, PAIR, TOKENS], F32)
-        gap = keep.tile([P, HALVES, PAIR, TOKENS], F32)
-        new_state = keep.tile([P, HALVES, PAIR, TOKENS], F32)
-        new_grouped = keep.tile([P, TOKENS, PACK], BF16, align_bytes=64)
-        out_1_flat = out_1.flatten_outer_dims()
+        def gate_function(i):
+            g, v = units[i]
+            nc.scalar.activation(out=gate_value[g][:, v], in_=gate_arg[i][:], func=TANH if g == GATE_N else SIGMOID)
 
-        products_r = [hidden_product(GATE_R, v) for v in range(HALVES)]
-        gi_r = gi_of_gate(GATE_R)
-        for v in range(HALVES):
-            arg = add_bias_then(ADD, GATE_R, v, products_r[v], gi_r[:, v])
-            nc.scalar.activation(out=reset[:, v], in_=arg[:], func=SIGMOID)
+        def after_function(i):
+            g, v = units[i]
+            if g == GATE_N:
+                nc.vector.tensor_tensor(out=gap[:, v], in0=old_state[:, v], in1=candidate[:, v], op=SUBTRACT)
+            if g == GATE_Z:
+                nc.vector.tensor_tensor(out=gap[:, v], in0=update[:, v], in1=gap[:, v], op=MULT)
+                nc.vector.tensor_tensor(out=new_state[:, v], in0=gap[:, v], in1=candidate[:, v], op=ADD)
+                nc.scalar.copy(
+                    out=new_grouped[:].rearrange("p t (v e) -> p v t e", e=PAIR)[:, v],
+                    in_=new_state[:, v].rearrange("p e t -> p t e"),
+                )
+                back[v] = flipped.tile([TOKENS, BANK_SLOTS, P], F32, tag="bank", name="back")
+                for e in range(PAIR):
+                    flip(back[v], e, new_state[:, v, e, :])
 
-        products_n = [hidden_product(GATE_N, v) for v in range(HALVES)]
-        gi_n = gi_of_gate(GATE_N)
-        for v in range(HALVES):
-            arg = add_bias_then(MULT, GATE_N, v, products_n[v], reset[:, v])
-            nc.vector.tensor_tensor(out=arg[:], in0=arg[:], in1=gi_n[:, v], op=ADD)
-            nc.scalar.activation(out=candidate[:, v], in_=arg[:], func=TANH)
-            nc.vector.tensor_tensor(out=gap[:, v], in0=old_state[:, v], in1=candidate[:, v], op=SUBTRACT)
+        def flip_gi(g):
+            gi_words = keep.tile([P, HALVES, TOKENS], F32, name="gi_words%d" % g)
+            nc.scalar.copy(out=gi_words[:], in_=flip_rows(gi_in[g]))
+            gi_values[g] = gi_words[:].bitcast(BF16).rearrange("p v (t e) -> p v e t", e=PAIR)
 
-        products_z = [hidden_product(GATE_Z, v) for v in range(HALVES)]
-        gi_z = gi_of_gate(GATE_Z)
-        for v in range(HALVES):
-            arg = add_bias_then(ADD, GATE_Z, v, products_z[v], gi_z[:, v])
-            nc.scalar.activation(out=arg[:], in_=arg[:], func=SIGMOID)
-            nc.vector.tensor_tensor(out=arg[:], in0=arg[:], in1=gap[:, v], op=MULT)
-            nc.vector.tensor_tensor(out=new_state[:, v], in0=arg[:], in1=candidate[:, v], op=ADD)
-            nc.scalar.copy(
-                out=new_grouped[:].rearrange("p t (v e) -> p v t e", e=PAIR)[:, v],
-                in_=new_state[:, v].rearrange("p e t -> p t e"),
-            )
+        def is_unit(i):
+            return 0 <= i < len(units)
 
-        wout_grouped, wout_operand = rows_to_operand(wout_in, "wout")
+        for i in range(len(units) + 4):
+            if is_unit(i):
+                flip_weights(i)
+            if is_unit(i - 1):
+                quantise_weights(i - 1)
+            if is_unit(i - 2):
+                gate_argument(i - 2)
+            if is_unit(i - 3):
+                gate_function(i - 3)
+            if is_unit(i) and units[i][1] == HALVES - 1:
+                flip_gi(units[i][0])
+            if i - 3 == len(units) - 1:
+                wout_grouped = regrouped(wout_in, "wout")
+            if is_unit(i - 4):
+                after_function(i - 4)
+
+        wout_operand = quantise(wout_grouped[:].rearrange("p m k -> p (m k)"), OUT, "wout")
         new_codes, new_scales = quantise(new_grouped[:].rearrange("p t k -> p (t k)"), TOKENS, "new")
         active = products.tile([TOKENS, OUT], F32, tag="product")
         multiply(active[:], (new_codes[:], new_scales[:]), wout_operand)
-        active_out = keep.tile([TOKENS, OUT], F32)
-        nc.vector.tensor_tensor(out=active_out[:], in0=active[:], in1=bout_all[:], op=ADD)
-        nc.sync.dma_start(out=out_0.flatten_outer_dims(), in_=active_out[:])
 
+        out_1_flat = out_1.flatten_outer_dims()
         for v in range(HALVES):
-            back = flipped.tile([TOKENS, BANK_SLOTS, P], F32, tag="bank")
-            for e in range(PAIR):
-                flip(back, e, new_state[:, v, e, :])
             new_out = per_unit.tile([TOKENS, P, PAIR], F32, name="new_out")
-            nc.scalar.copy(out=new_out[:], in_=back[:, 0:PAIR, :].rearrange("t e p -> t p e"))
+            nc.scalar.copy(out=new_out[:], in_=back[v][:, 0:PAIR, :].rearrange("t e p -> t p e"))
             nc.sync.dma_start(
                 out=out_1_flat[:, v * PAIR * P : (v + 1) * PAIR * P], in_=new_out[:].rearrange("t p e -> t (p e)")
             )
+
+        active_out = keep.tile([TOKENS, OUT], F32)
+        nc.vector.tensor_tensor(out=active_out[:], in0=active[:], in1=bout_all[:], op=ADD)
+        nc.sync.dma_start(out=out_0.flatten_outer_dims(), in_=active_out[:])

@@ -39,11 +39,12 @@ def tile_vectorizednpu_pb_s_kernel(tc, gi, registers, W_hh, b_hh, W_out, b_out, 
         flipped = ctx.enter_context(tc.psum_pool(name="flipped", bufs=5))
         products = ctx.enter_context(tc.psum_pool(name="products", bufs=3))
 
+        identity = keep.tile([P, P], F32)
+        make_identity(nc, identity[:])
+
         regs_in = keep.tile([TOKENS, STATE], BF16)
-        nc.sync.dma_start(out=regs_in[:], in_=registers.flatten_outer_dims())
         bias_rows = keep.tile([P, HALVES * P], BF16)
         nc.vector.memset(bias_rows[:], 0.0)
-        nc.sync.dma_start(out=bias_rows[0 : GATES * HALVES, :], in_=b_hh.rearrange("(r c) -> r c", c=HALVES * P))
         w_view = W_hh.rearrange("(g v p e) k -> g v p e k", g=GATES, v=HALVES, p=P, e=PAIR)
         gi_flat = gi.flatten_outer_dims()
         gi_in = {}
@@ -52,6 +53,12 @@ def tile_vectorizednpu_pb_s_kernel(tc, gi, registers, W_hh, b_hh, W_out, b_out, 
             for v in range(HALVES):
                 w_rows[(g, v)] = per_unit.tile([P, PAIR, STATE], BF16, name="w_rows")
                 nc.sync.dma_start(out=w_rows[(g, v)][:], in_=w_view[g, v])
+                if (g, v) == units[0]:
+                    nc.sync.dma_start(out=regs_in[:], in_=registers.flatten_outer_dims())
+                if (g, v) == units[1]:
+                    bias_view = b_hh.rearrange("(r c) -> r c", c=HALVES * P)
+                    for rows in (slice(0, 4), slice(4, GATES * HALVES)):
+                        nc.sync.dma_start(out=bias_rows[rows, :], in_=bias_view[rows, :])
             gi_in[g] = keep.tile([TOKENS, STATE], BF16, name="gi_in%d" % g)
             nc.sync.dma_start(out=gi_in[g][:], in_=gi_flat[:, g * STATE : (g + 1) * STATE])
         wout_in = keep.tile([OUT, STATE], BF16)
@@ -59,8 +66,6 @@ def tile_vectorizednpu_pb_s_kernel(tc, gi, registers, W_hh, b_hh, W_out, b_out, 
         bout_all = keep.tile([P, OUT], BF16)
         nc.sync.dma_start(out=bout_all[:], in_=b_out.partition_broadcast(P))
 
-        identity = keep.tile([P, P], F32)
-        make_identity(nc, identity[:])
         warm = keep.tile([P, 1], F32)
         nc.vector.memset(warm[:], 0.0)
         nc.scalar.activation(out=warm[:], in_=warm[:], func=SIGMOID)
@@ -96,16 +101,6 @@ def tile_vectorizednpu_pb_s_kernel(tc, gi, registers, W_hh, b_hh, W_out, b_out, 
                 start=True,
                 stop=True,
             )
-
-        reg_grouped = regrouped(regs_in, "reg")
-        old_state = reg_grouped[:].rearrange("p t (v e) -> p v e t", e=PAIR)
-        bias_bank = flipped.tile([P, BANK_SLOTS, P], F32, tag="bank")
-        flip(bias_bank, 0, bias_rows[:].bitcast(F32))
-        bias = keep.tile([P, GATES * HALVES, PAIR], F32)
-        nc.vector.tensor_copy(
-            out=bias[:].rearrange("p r e -> p (r e)"), in_=bias_bank[:, 0, 0 : GATES * HALVES].bitcast(BF16)
-        )
-        reg_operand = quantise(reg_grouped[:].rearrange("p m k -> p (m k)"), TOKENS, "reg")
 
         gi_values = {}
         w_grouped = {}
@@ -183,8 +178,19 @@ def tile_vectorizednpu_pb_s_kernel(tc, gi, registers, W_hh, b_hh, W_out, b_out, 
         for i in range(len(units) + 4):
             if is_unit(i):
                 flip_weights(i)
+            if i == 0:
+                reg_grouped = regrouped(regs_in, "reg")
+                old_state = reg_grouped[:].rearrange("p t (v e) -> p v e t", e=PAIR)
             if is_unit(i - 1):
                 quantise_weights(i - 1)
+            if i == 1:
+                bias_bank = flipped.tile([P, BANK_SLOTS, P], F32, tag="bank")
+                flip(bias_bank, 0, bias_rows[:].bitcast(F32))
+                bias = keep.tile([P, GATES * HALVES, PAIR], F32)
+                nc.vector.tensor_copy(
+                    out=bias[:].rearrange("p r e -> p (r e)"), in_=bias_bank[:, 0, 0 : GATES * HALVES].bitcast(BF16)
+                )
+                reg_operand = quantise(reg_grouped[:].rearrange("p m k -> p (m k)"), TOKENS, "reg")
             if is_unit(i - 2):
                 gate_argument(i - 2)
             if is_unit(i - 3):

@@ -42,12 +42,19 @@ def tile_vectorizednpu_pb_s_kernel(tc, gi, registers, W_hh, b_hh, W_out, b_out, 
         identity = keep.tile([P, P], F32)
         make_identity(nc, identity[:])
 
+        zeros = keep.tile([P, P], F32)
+        nc.vector.memset(zeros[:], 0.0)
+
         regs_in = keep.tile([TOKENS, STATE], BF16)
         bias_rows = keep.tile([P, HALVES * P], BF16)
         nc.vector.memset(bias_rows[:], 0.0)
         w_view = W_hh.rearrange("(g v p e) k -> g v p e k", g=GATES, v=HALVES, p=P, e=PAIR)
         gi_flat = gi.flatten_outer_dims()
         gi_in = {}
+
+        def load_gi(g):
+            nc.sync.dma_start(out=gi_in[g][:], in_=gi_flat[:, g * STATE : (g + 1) * STATE])
+
         w_rows = {}
         for g in GATE_ORDER:
             for v in range(HALVES):
@@ -60,15 +67,20 @@ def tile_vectorizednpu_pb_s_kernel(tc, gi, registers, W_hh, b_hh, W_out, b_out, 
                     for rows in (slice(0, 4), slice(4, GATES * HALVES)):
                         nc.sync.dma_start(out=bias_rows[rows, :], in_=bias_view[rows, :])
             gi_in[g] = keep.tile([TOKENS, STATE], BF16, name="gi_in%d" % g)
-            nc.sync.dma_start(out=gi_in[g][:], in_=gi_flat[:, g * STATE : (g + 1) * STATE])
+            if g == GATE_R:
+                load_gi(g)
+        for g in (GATE_N, GATE_Z):
+            load_gi(g)
         wout_in = keep.tile([OUT, STATE], BF16)
         nc.sync.dma_start(out=wout_in[:], in_=W_out)
         bout_all = keep.tile([P, OUT], BF16)
         nc.sync.dma_start(out=bout_all[:], in_=b_out.partition_broadcast(P))
 
-        warm = keep.tile([P, 1], F32)
-        nc.vector.memset(warm[:], 0.0)
-        nc.scalar.activation(out=warm[:], in_=warm[:], func=SIGMOID)
+        table = keep.tile([P, 1], F32)
+        nc.scalar.activation(out=table[:], in_=zeros[:, 0:1], func=SIGMOID)
+        idle = flipped.tile([P, BANK_SLOTS, P], F32, tag="bank")
+        for slot in range(BANK_SLOTS - 1):
+            nc.tensor.matmul(out=idle[:, slot, :], lhsT=zeros[:], rhs=zeros[:], start=True, stop=True)
 
         def flip(bank, slot, words):
             nc.tensor.transpose(out=bank[:, slot, :], in_=words, identity=identity[:])
@@ -105,6 +117,7 @@ def tile_vectorizednpu_pb_s_kernel(tc, gi, registers, W_hh, b_hh, W_out, b_out, 
         gi_values = {}
         w_grouped = {}
         w_operand = {}
+        gh = {}
         gate_arg = {}
         back = {}
         reset = keep.tile([P, HALVES, PAIR, TOKENS], F32)
@@ -114,6 +127,7 @@ def tile_vectorizednpu_pb_s_kernel(tc, gi, registers, W_hh, b_hh, W_out, b_out, 
         gap = keep.tile([P, HALVES, PAIR, TOKENS], F32)
         new_state = keep.tile([P, HALVES, PAIR, TOKENS], F32)
         new_grouped = keep.tile([P, TOKENS, PACK], BF16, align_bytes=64)
+        new_places = new_grouped[:].rearrange("p t (v e) -> p v t e", e=PAIR)
 
         def flip_weights(i):
             words = w_rows[units[i]][:].bitcast(F32)
@@ -124,85 +138,122 @@ def tile_vectorizednpu_pb_s_kernel(tc, gi, registers, W_hh, b_hh, W_out, b_out, 
             w_grouped[i] = per_unit.tile([P, PAIR, P, PACK], BF16, align_bytes=64, name="w_grouped")
             nc.scalar.copy(out=w_grouped[i][:].bitcast(F32), in_=bank[:].rearrange("p (e h) m -> p e m h", h=HALVES))
 
+        def flip_gi(g, copy):
+            gi_words = keep.tile([P, HALVES, TOKENS], F32, name="gi_words%d" % g)
+            copy(out=gi_words[:], in_=flip_rows(gi_in[g]))
+            gi_values[g] = gi_words[:].bitcast(BF16).rearrange("p v (t e) -> p v e t", e=PAIR)
+
         def quantise_weights(i):
             w_operand[i] = quantise(w_grouped[i][:].rearrange("p e m k -> p (e m k)"), PAIR * P, "w")
 
-        def gate_argument(i):
-            g, v = units[i]
+        def multiply_unit(i):
             w_codes, w_scales = w_operand[i]
-            gh = products.tile([P, PAIR, TOKENS], F32, tag="product")
+            gh[i] = products.tile([P, PAIR, TOKENS], F32, tag="product", name="gh")
             for e in range(PAIR):
                 rows = slice(e * P, (e + 1) * P)
-                multiply(gh[:, e, :], (w_codes[:, rows], w_scales[:, rows]), reg_operand)
+                multiply(gh[i][:, e, :], (w_codes[:, rows], w_scales[:, rows]), reg_operand)
+
+        def gate_argument(i):
+            g, v = units[i]
             other, op = (reset[:, v], MULT) if g == GATE_N else (gi_values[g][:, v], ADD)
             gate_arg[i] = per_unit.tile([P, PAIR, TOKENS], F32, name="gate_arg")
             for e in range(PAIR):
                 nc.vector.scalar_tensor_tensor(
                     out=gate_arg[i][:, e, :],
-                    in0=gh[:, e, :],
+                    in0=gh[i][:, e, :],
                     scalar=bias[:, HALVES * g + v, e : e + 1],
                     in1=other[:, e, :],
                     op0=ADD,
                     op1=op,
                 )
-            if g == GATE_N:
-                nc.vector.tensor_tensor(out=gate_arg[i][:], in0=gate_arg[i][:], in1=gi_values[g][:, v], op=ADD)
+
+        def add_gi(i):
+            g, v = units[i]
+            nc.vector.tensor_tensor(out=gate_arg[i][:], in0=gate_arg[i][:], in1=gi_values[g][:, v], op=ADD)
 
         def gate_function(i):
             g, v = units[i]
             nc.scalar.activation(out=gate_value[g][:, v], in_=gate_arg[i][:], func=TANH if g == GATE_N else SIGMOID)
 
-        def after_function(i):
-            g, v = units[i]
-            if g == GATE_N:
-                nc.vector.tensor_tensor(out=gap[:, v], in0=old_state[:, v], in1=candidate[:, v], op=SUBTRACT)
-            if g == GATE_Z:
-                nc.vector.tensor_tensor(out=gap[:, v], in0=update[:, v], in1=gap[:, v], op=MULT)
-                nc.vector.tensor_tensor(out=new_state[:, v], in0=gap[:, v], in1=candidate[:, v], op=ADD)
-                nc.scalar.copy(
-                    out=new_grouped[:].rearrange("p t (v e) -> p v t e", e=PAIR)[:, v],
-                    in_=new_state[:, v].rearrange("p e t -> p t e"),
-                )
-                back[v] = flipped.tile([TOKENS, BANK_SLOTS, P], F32, tag="bank", name="back")
-                for e in range(PAIR):
-                    flip(back[v], e, new_state[:, v, e, :])
+        def subtract_candidate(v):
+            nc.vector.tensor_tensor(out=gap[:, v], in0=old_state[:, v], in1=candidate[:, v], op=SUBTRACT)
 
-        def flip_gi(g):
-            gi_words = keep.tile([P, HALVES, TOKENS], F32, name="gi_words%d" % g)
-            nc.scalar.copy(out=gi_words[:], in_=flip_rows(gi_in[g]))
-            gi_values[g] = gi_words[:].bitcast(BF16).rearrange("p v (t e) -> p v e t", e=PAIR)
+        def scale_gap(v):
+            nc.vector.tensor_tensor(out=gap[:, v], in0=update[:, v], in1=gap[:, v], op=MULT)
 
-        def is_unit(i):
-            return 0 <= i < len(units)
+        def add_candidate(v):
+            nc.vector.tensor_tensor(out=new_state[:, v], in0=gap[:, v], in1=candidate[:, v], op=ADD)
 
-        for i in range(len(units) + 4):
-            if is_unit(i):
-                flip_weights(i)
-            if i == 0:
-                reg_grouped = regrouped(regs_in, "reg")
-                old_state = reg_grouped[:].rearrange("p t (v e) -> p v e t", e=PAIR)
-            if is_unit(i - 1):
-                quantise_weights(i - 1)
-            if i == 1:
-                bias_bank = flipped.tile([P, BANK_SLOTS, P], F32, tag="bank")
-                flip(bias_bank, 0, bias_rows[:].bitcast(F32))
-                bias = keep.tile([P, GATES * HALVES, PAIR], F32)
-                nc.vector.tensor_copy(
-                    out=bias[:].rearrange("p r e -> p (r e)"), in_=bias_bank[:, 0, 0 : GATES * HALVES].bitcast(BF16)
-                )
-                reg_operand = quantise(reg_grouped[:].rearrange("p m k -> p (m k)"), TOKENS, "reg")
-            if is_unit(i - 2):
-                gate_argument(i - 2)
-            if is_unit(i - 3):
-                gate_function(i - 3)
-            if is_unit(i) and units[i][1] == HALVES - 1:
-                flip_gi(units[i][0])
-            if i - 3 == len(units) - 1:
-                wout_grouped = regrouped(wout_in, "wout")
-            if is_unit(i - 4):
-                after_function(i - 4)
+        def flip_back(v):
+            back[v] = flipped.tile([TOKENS, BANK_SLOTS, P], F32, tag="bank", name="back")
+            for e in range(PAIR):
+                flip(back[v], e, new_state[:, v, e, :])
 
+        R0, R1, N0, N1, Z0, Z1 = range(len(units))
+
+        flip_weights(R0)
+        reg_grouped = regrouped(regs_in, "reg")
+        old_state = reg_grouped[:].rearrange("p t (v e) -> p v e t", e=PAIR)
+        flip_weights(R1)
+        quantise_weights(R0)
+        bias_bank = flipped.tile([P, BANK_SLOTS, P], F32, tag="bank")
+        flip(bias_bank, 0, bias_rows[:].bitcast(F32))
+        bias = keep.tile([P, GATES * HALVES, PAIR], F32)
+        nc.vector.tensor_copy(
+            out=bias[:].rearrange("p r e -> p (r e)"), in_=bias_bank[:, 0, 0 : GATES * HALVES].bitcast(BF16)
+        )
+        reg_operand = quantise(reg_grouped[:].rearrange("p m k -> p (m k)"), TOKENS, "reg")
+        flip_gi(GATE_R, nc.vector.tensor_copy)
+        flip_weights(N0)
+        multiply_unit(R0)
+        quantise_weights(R1)
+        gate_argument(R0)
+        flip_weights(N1)
+        multiply_unit(R1)
+        quantise_weights(N0)
+        gate_argument(R1)
+        gate_function(R0)
+        flip_weights(Z0)
+        flip_weights(Z1)
+        quantise_weights(N1)
+        flip_gi(GATE_N, nc.vector.tensor_copy)
+        multiply_unit(N0)
+        gate_argument(N0)
+        gate_function(R1)
+        quantise_weights(Z0)
+        multiply_unit(N1)
+        add_gi(N0)
+        flip_gi(GATE_Z, nc.scalar.copy)
+        gate_argument(N1)
+        gate_function(N0)
+        wout_grouped = regrouped(wout_in, "wout")
+        quantise_weights(Z1)
+        add_gi(N1)
+        multiply_unit(Z0)
+        gate_argument(Z0)
+        gate_function(N1)
+        multiply_unit(Z1)
+        gate_argument(Z1)
+        gate_function(Z0)
+        gate_function(Z1)
+        for v in range(HALVES):
+            subtract_candidate(v)
         wout_operand = quantise(wout_grouped[:].rearrange("p m k -> p (m k)"), OUT, "wout")
+        for v in range(HALVES):
+            scale_gap(v)
+
+        add_candidate(0)
+        nc.scalar.copy(out=new_places[:, 0], in_=new_state[:, 0].rearrange("p e t -> p t e"))
+        flip_back(0)
+        nc.vector.tensor_tensor(
+            out=new_places[:, 1],
+            in0=gap[:, 1].rearrange("p e t -> p t e"),
+            in1=candidate[:, 1].rearrange("p e t -> p t e"),
+            op=ADD,
+        )
+        add_candidate(1)
+        flip_back(1)
+
         new_codes, new_scales = quantise(new_grouped[:].rearrange("p t k -> p (t k)"), TOKENS, "new")
         active = products.tile([TOKENS, OUT], F32, tag="product")
         multiply(active[:], (new_codes[:], new_scales[:]), wout_operand)

@@ -59,7 +59,11 @@ def tile_vectorizednpu_pb_s_kernel(tc, gi, registers, W_hh, b_hh, W_out, b_out, 
         for g in GATE_ORDER:
             for v in range(HALVES):
                 w_rows[(g, v)] = per_unit.tile([P, PAIR, STATE], BF16, name="w_rows")
-                nc.sync.dma_start(out=w_rows[(g, v)][:], in_=w_view[g, v])
+                if (g, v) == units[0]:
+                    for e in range(PAIR):
+                        nc.sync.dma_start(out=w_rows[(g, v)][:, e, :], in_=w_view[g, v, :, e, :])
+                else:
+                    nc.sync.dma_start(out=w_rows[(g, v)][:], in_=w_view[g, v])
                 if (g, v) == units[0]:
                     nc.sync.dma_start(out=regs_in[:], in_=registers.flatten_outer_dims())
                 if (g, v) == units[1]:
@@ -86,16 +90,25 @@ def tile_vectorizednpu_pb_s_kernel(tc, gi, registers, W_hh, b_hh, W_out, b_out, 
             nc.tensor.transpose(out=bank[:, slot, :], in_=words, identity=identity[:])
 
         def flip_rows(rows_in):
-            words = rows_in[:].bitcast(F32)
+            return flip_words(rows_in[:].bitcast(F32))
+
+        def flip_words(words):
             bank = flipped.tile([P, BANK_SLOTS, P], F32, tag="bank")
             for v in range(HALVES):
                 flip(bank, v, words[:, v * P : (v + 1) * P])
             return bank[:, 0:HALVES, :]
 
-        def quantise(grouped, width, name):
+        def quantise(grouped, width, name, parts=1):
             codes = per_unit.tile([P, width], U32, align_bytes=64, name=name + "_codes")
             scales = per_unit.tile([P, width], U8, align_bytes=64, name=name + "_scales")
-            nc.vector.quantize_mx(out=codes[:].bitcast(FP8X4), scales=scales[:], in_=grouped)
+            part = width // parts
+            for first in range(0, width, part):
+                columns = slice(first, first + part)
+                nc.vector.quantize_mx(
+                    out=codes[:, columns].bitcast(FP8X4),
+                    scales=scales[:, columns],
+                    in_=grouped[:, first * PACK : (first + part) * PACK],
+                )
             return codes, scales
 
         def regrouped(rows_in, name):
@@ -138,13 +151,20 @@ def tile_vectorizednpu_pb_s_kernel(tc, gi, registers, W_hh, b_hh, W_out, b_out, 
             w_grouped[i] = per_unit.tile([P, PAIR, P, PACK], BF16, align_bytes=64, name="w_grouped")
             nc.scalar.copy(out=w_grouped[i][:].bitcast(F32), in_=bank[:].rearrange("p (e h) m -> p e m h", h=HALVES))
 
+        def flip_half(i, e):
+            if e == 0:
+                w_grouped[i] = per_unit.tile([P, PAIR, P, PACK], BF16, align_bytes=64, name="w_grouped")
+            bank = flip_words(w_rows[units[i]][:, e, :].bitcast(F32))
+            nc.scalar.copy(out=w_grouped[i][:, e].bitcast(F32), in_=bank.rearrange("p h m -> p m h"))
+
         def flip_gi(g, copy):
             gi_words = keep.tile([P, HALVES, TOKENS], F32, name="gi_words%d" % g)
             copy(out=gi_words[:], in_=flip_rows(gi_in[g]))
             gi_values[g] = gi_words[:].bitcast(BF16).rearrange("p v (t e) -> p v e t", e=PAIR)
 
-        def quantise_weights(i):
-            w_operand[i] = quantise(w_grouped[i][:].rearrange("p e m k -> p (e m k)"), PAIR * P, "w")
+        def quantise_weights(i, parts=1):
+            grouped = w_grouped[i][:].rearrange("p e m k -> p (e m k)")
+            w_operand[i] = quantise(grouped, PAIR * P, "w", parts)
 
         def multiply_unit(i):
             w_codes, w_scales = w_operand[i]
@@ -191,11 +211,12 @@ def tile_vectorizednpu_pb_s_kernel(tc, gi, registers, W_hh, b_hh, W_out, b_out, 
 
         R0, R1, N0, N1, Z0, Z1 = range(len(units))
 
-        flip_weights(R0)
+        for e in range(PAIR):
+            flip_half(R0, e)
         reg_grouped = regrouped(regs_in, "reg")
         old_state = reg_grouped[:].rearrange("p t (v e) -> p v e t", e=PAIR)
         flip_weights(R1)
-        quantise_weights(R0)
+        quantise_weights(R0, parts=PAIR)
         bias_bank = flipped.tile([P, BANK_SLOTS, P], F32, tag="bank")
         flip(bias_bank, 0, bias_rows[:].bitcast(F32))
         bias = keep.tile([P, GATES * HALVES, PAIR], F32)
@@ -262,7 +283,8 @@ def tile_vectorizednpu_pb_s_kernel(tc, gi, registers, W_hh, b_hh, W_out, b_out, 
         for v in range(HALVES):
             new_out = per_unit.tile([TOKENS, P, PAIR], F32, name="new_out")
             nc.scalar.copy(out=new_out[:], in_=back[v][:, 0:PAIR, :].rearrange("t e p -> t p e"))
-            nc.sync.dma_start(
+            queue = (nc.sync, nc.scalar)[v]
+            queue.dma_start(
                 out=out_1_flat[:, v * PAIR * P : (v + 1) * PAIR * P], in_=new_out[:].rearrange("t p e -> t (p e)")
             )
 

@@ -24,6 +24,8 @@ PACK = HALVES * PAIR
 GATES = 3
 GATE_R, GATE_Z, GATE_N = 0, 1, 2
 GATE_ORDER = (GATE_R, GATE_N, GATE_Z)
+BIAS_ROWS = 2
+BIAS_BLOCKS = GATES * HALVES // BIAS_ROWS
 BANK_SLOTS = 4
 
 FLOPS = 2 * TOKENS * STATE * (GATES * STATE + OUT)
@@ -37,7 +39,8 @@ def tile_vectorizednpu_pb_s_kernel(tc, gi, registers, W_hh, b_hh, W_out, b_out, 
         keep = ctx.enter_context(tc.tile_pool(name="keep", bufs=1))
         per_unit = ctx.enter_context(tc.tile_pool(name="per_unit", bufs=GATES * HALVES))
         flipped = ctx.enter_context(tc.psum_pool(name="flipped", bufs=5))
-        products = ctx.enter_context(tc.psum_pool(name="products", bufs=3))
+        products = ctx.enter_context(tc.psum_pool(name="products", bufs=2))
+        unread = ctx.enter_context(tc.psum_pool(name="unread", bufs=1))
 
         identity = keep.tile([P, P], F32)
         make_identity(nc, identity[:])
@@ -46,7 +49,7 @@ def tile_vectorizednpu_pb_s_kernel(tc, gi, registers, W_hh, b_hh, W_out, b_out, 
         nc.vector.memset(zeros[:], 0.0)
 
         regs_in = keep.tile([TOKENS, STATE], BF16)
-        bias_rows = keep.tile([P, HALVES * P], BF16)
+        bias_rows = keep.tile([P, BIAS_BLOCKS * HALVES * P], BF16)
         nc.vector.memset(bias_rows[:], 0.0)
         w_view = W_hh.rearrange("(g v p e) k -> g v p e k", g=GATES, v=HALVES, p=P, e=PAIR)
         gi_flat = gi.flatten_outer_dims()
@@ -67,9 +70,7 @@ def tile_vectorizednpu_pb_s_kernel(tc, gi, registers, W_hh, b_hh, W_out, b_out, 
                 if (g, v) == units[0]:
                     nc.sync.dma_start(out=regs_in[:], in_=registers.flatten_outer_dims())
                 if (g, v) == units[1]:
-                    bias_view = b_hh.rearrange("(r c) -> r c", c=HALVES * P)
-                    for rows in (slice(0, 4), slice(4, GATES * HALVES)):
-                        nc.sync.dma_start(out=bias_rows[rows, :], in_=bias_view[rows, :])
+                    nc.sync.dma_start(out=bias_rows[0:BIAS_ROWS, :], in_=b_hh.rearrange("(r c) -> r c", r=BIAS_ROWS))
             gi_in[g] = keep.tile([TOKENS, STATE], BF16, name="gi_in%d" % g)
             if g == GATE_R:
                 load_gi(g)
@@ -82,9 +83,13 @@ def tile_vectorizednpu_pb_s_kernel(tc, gi, registers, W_hh, b_hh, W_out, b_out, 
 
         table = keep.tile([P, 1], F32)
         nc.scalar.activation(out=table[:], in_=zeros[:, 0:1], func=SIGMOID)
-        idle = flipped.tile([P, BANK_SLOTS, P], F32, tag="bank")
-        for slot in range(BANK_SLOTS - 1):
-            nc.tensor.matmul(out=idle[:, slot, :], lhsT=zeros[:], rhs=zeros[:], start=True, stop=True)
+        idle = unread.tile([P, PAIR * P], F32)
+
+        def multiply_zeros(columns):
+            nc.tensor.matmul(out=idle[:, 0:columns], lhsT=zeros[:], rhs=zeros[:, 0:columns], start=True, stop=True)
+
+        for n in range(3):
+            multiply_zeros(P)
 
         def flip(bank, slot, words):
             nc.tensor.transpose(out=bank[:, slot, :], in_=words, identity=identity[:])
@@ -166,6 +171,11 @@ def tile_vectorizednpu_pb_s_kernel(tc, gi, registers, W_hh, b_hh, W_out, b_out, 
             grouped = w_grouped[i][:].rearrange("p e m k -> p (e m k)")
             w_operand[i] = quantise(grouped, PAIR * P, "w", parts)
 
+        def multiply_codes(i, times):
+            w_codes, w_scales = w_operand[i]
+            for n in range(times):
+                multiply(idle[:], (w_codes[:, 0:P], w_scales[:, 0:P]), (w_codes, w_scales))
+
         def multiply_unit(i):
             w_codes, w_scales = w_operand[i]
             gh[i] = products.tile([P, PAIR, TOKENS], F32, tag="product", name="gh")
@@ -214,18 +224,24 @@ def tile_vectorizednpu_pb_s_kernel(tc, gi, registers, W_hh, b_hh, W_out, b_out, 
         for e in range(PAIR):
             flip_half(R0, e)
         reg_grouped = regrouped(regs_in, "reg")
+        multiply_zeros(P // 2)
         old_state = reg_grouped[:].rearrange("p t (v e) -> p v e t", e=PAIR)
         flip_weights(R1)
+        multiply_zeros(P // 2)
         quantise_weights(R0, parts=PAIR)
         bias_bank = flipped.tile([P, BANK_SLOTS, P], F32, tag="bank")
-        flip(bias_bank, 0, bias_rows[:].bitcast(F32))
+        for c in range(BIAS_BLOCKS):
+            flip(bias_bank, c, bias_rows[:, c * HALVES * P : (c + 1) * HALVES * P].bitcast(F32))
         bias = keep.tile([P, GATES * HALVES, PAIR], F32)
         nc.vector.tensor_copy(
-            out=bias[:].rearrange("p r e -> p (r e)"), in_=bias_bank[:, 0, 0 : GATES * HALVES].bitcast(BF16)
+            out=bias[:].rearrange("p (r c) e -> p c r e", r=BIAS_ROWS),
+            in_=bias_bank[:, 0:BIAS_BLOCKS, 0:BIAS_ROWS].bitcast(BF16).rearrange("p c (r e) -> p c r e", e=PAIR),
         )
         reg_operand = quantise(reg_grouped[:].rearrange("p m k -> p (m k)"), TOKENS, "reg")
         flip_gi(GATE_R, nc.vector.tensor_copy)
+        multiply_zeros(P // 2)
         flip_weights(N0)
+        multiply_zeros(P // 2)
         multiply_unit(R0)
         quantise_weights(R1)
         gate_argument(R0)
@@ -254,27 +270,28 @@ def tile_vectorizednpu_pb_s_kernel(tc, gi, registers, W_hh, b_hh, W_out, b_out, 
         gate_argument(Z0)
         gate_function(N1)
         multiply_unit(Z1)
+        multiply_codes(Z1, 6)
         gate_argument(Z1)
         gate_function(Z0)
         gate_function(Z1)
         for v in range(HALVES):
             subtract_candidate(v)
-        wout_operand = quantise(wout_grouped[:].rearrange("p m k -> p (m k)"), OUT, "wout")
         for v in range(HALVES):
             scale_gap(v)
 
         add_candidate(0)
         nc.scalar.copy(out=new_places[:, 0], in_=new_state[:, 0].rearrange("p e t -> p t e"))
         flip_back(0)
+        add_candidate(1)
+        flip_back(1)
         nc.vector.tensor_tensor(
             out=new_places[:, 1],
             in0=gap[:, 1].rearrange("p e t -> p t e"),
             in1=candidate[:, 1].rearrange("p e t -> p t e"),
             op=ADD,
         )
-        add_candidate(1)
-        flip_back(1)
 
+        wout_operand = quantise(wout_grouped[:].rearrange("p m k -> p (m k)"), OUT, "wout")
         new_codes, new_scales = quantise(new_grouped[:].rearrange("p t k -> p (t k)"), TOKENS, "new")
         active = products.tile([TOKENS, OUT], F32, tag="product")
         multiply(active[:], (new_codes[:], new_scales[:]), wout_operand)

@@ -116,9 +116,9 @@ def tile_vectorizednpu_pb_s_kernel(tc, gi, registers, W_hh, b_hh, W_out, b_out, 
                 )
             return codes, scales
 
-        def regrouped(rows_in, name):
+        def regrouped(flipped_rows, name):
             grouped = keep.tile([P, P, PACK], BF16, align_bytes=64, name=name + "_grouped")
-            nc.scalar.copy(out=grouped[:].bitcast(F32), in_=flip_rows(rows_in).rearrange("p v m -> p m v"))
+            nc.scalar.copy(out=grouped[:].bitcast(F32), in_=flipped_rows.rearrange("p v m -> p m v"))
             return grouped
 
         def multiply(out, stationary, moving):
@@ -223,7 +223,7 @@ def tile_vectorizednpu_pb_s_kernel(tc, gi, registers, W_hh, b_hh, W_out, b_out, 
 
         for e in range(PAIR):
             flip_half(R0, e)
-        reg_grouped = regrouped(regs_in, "reg")
+        reg_grouped = regrouped(flip_rows(regs_in), "reg")
         multiply_zeros(P // 2)
         old_state = reg_grouped[:].rearrange("p t (v e) -> p v e t", e=PAIR)
         flip_weights(R1)
@@ -242,38 +242,39 @@ def tile_vectorizednpu_pb_s_kernel(tc, gi, registers, W_hh, b_hh, W_out, b_out, 
         multiply_zeros(P // 2)
         flip_weights(N0)
         multiply_zeros(P // 2)
-        multiply_unit(R0)
         quantise_weights(R1)
-        gate_argument(R0)
         flip_weights(N1)
+        multiply_unit(R0)
+        gate_argument(R0)
         multiply_unit(R1)
-        quantise_weights(N0)
         gate_argument(R1)
-        gate_function(R0)
+        quantise_weights(N0)
         flip_weights(Z0)
+        gate_function(R0)
         flip_weights(Z1)
         quantise_weights(N1)
-        flip_gi(GATE_N, nc.vector.tensor_copy)
-        multiply_unit(N0)
-        gate_argument(N0)
         gate_function(R1)
-        quantise_weights(Z0)
-        multiply_unit(N1)
-        add_gi(N0)
+        flip_gi(GATE_N, nc.vector.tensor_copy)
         flip_gi(GATE_Z, nc.scalar.copy)
-        gate_argument(N1)
-        gate_function(N0)
-        wout_grouped = regrouped(wout_in, "wout")
+        wout_flipped = flip_rows(wout_in)
+        multiply_unit(N0)
+        multiply_unit(N1)
+        quantise_weights(Z0)
+        gate_argument(N0)
         quantise_weights(Z1)
+        gate_argument(N1)
+        add_gi(N0)
+        gate_function(N0)
         add_gi(N1)
-        multiply_unit(Z0)
-        gate_argument(Z0)
         gate_function(N1)
+        multiply_unit(Z0)
         multiply_unit(Z1)
         multiply_codes(Z1, 6)
-        gate_argument(Z1)
+        gate_argument(Z0)
         gate_function(Z0)
+        gate_argument(Z1)
         gate_function(Z1)
+        wout_grouped = regrouped(wout_flipped, "wout")
         for v in range(HALVES):
             subtract_candidate(v)
         for v in range(HALVES):

@@ -26,6 +26,7 @@ GATE_R, GATE_Z, GATE_N = 0, 1, 2
 GATE_ORDER = (GATE_R, GATE_N, GATE_Z)
 BIAS_ROWS = 2
 BIAS_BLOCKS = GATES * HALVES // BIAS_ROWS
+LINE = 4
 BANK_SLOTS = 4
 
 FLOPS = 2 * TOKENS * STATE * (GATES * STATE + OUT)
@@ -143,9 +144,7 @@ def tile_vectorizednpu_pb_s_kernel(tc, gi, registers, W_hh, b_hh, W_out, b_out, 
         update = keep.tile([P, HALVES, PAIR, TOKENS], F32)
         gate_value = {GATE_R: reset, GATE_N: candidate, GATE_Z: update}
         gap = keep.tile([P, HALVES, PAIR, TOKENS], F32)
-        new_state = keep.tile([P, HALVES, PAIR, TOKENS], F32)
         new_grouped = keep.tile([P, TOKENS, PACK], BF16, align_bytes=64)
-        new_places = new_grouped[:].rearrange("p t (v e) -> p v t e", e=PAIR)
 
         def flip_weights(i):
             words = w_rows[units[i]][:].bitcast(F32)
@@ -211,13 +210,18 @@ def tile_vectorizednpu_pb_s_kernel(tc, gi, registers, W_hh, b_hh, W_out, b_out, 
         def scale_gap(v):
             nc.vector.tensor_tensor(out=gap[:, v], in0=update[:, v], in1=gap[:, v], op=MULT)
 
-        def add_candidate(v):
-            nc.vector.tensor_tensor(out=new_state[:, v], in0=gap[:, v], in1=candidate[:, v], op=ADD)
-
         def flip_back(v):
             back[v] = flipped.tile([TOKENS, BANK_SLOTS, P], F32, tag="bank", name="back")
             for e in range(PAIR):
-                flip(back[v], e, new_state[:, v, e, :])
+                for term, first in ((candidate, True), (gap, False)):
+                    nc.tensor.matmul(
+                        out=back[v][:, e, :],
+                        lhsT=term[:, v, e, :],
+                        rhs=identity[:],
+                        is_transpose=True,
+                        start=first,
+                        stop=not first,
+                    )
 
         R0, R1, N0, N1, Z0, Z1 = range(len(units))
 
@@ -241,11 +245,10 @@ def tile_vectorizednpu_pb_s_kernel(tc, gi, registers, W_hh, b_hh, W_out, b_out, 
         flip_gi(GATE_R, nc.vector.tensor_copy)
         multiply_zeros(P // 2)
         flip_weights(N0)
-        multiply_zeros(P // 2)
         quantise_weights(R1)
-        flip_weights(N1)
         multiply_unit(R0)
         gate_argument(R0)
+        flip_weights(N1)
         multiply_unit(R1)
         gate_argument(R1)
         quantise_weights(N0)
@@ -280,19 +283,16 @@ def tile_vectorizednpu_pb_s_kernel(tc, gi, registers, W_hh, b_hh, W_out, b_out, 
         for v in range(HALVES):
             scale_gap(v)
 
-        add_candidate(0)
-        nc.scalar.copy(out=new_places[:, 0], in_=new_state[:, 0].rearrange("p e t -> p t e"))
-        flip_back(0)
-        add_candidate(1)
-        flip_back(1)
+        for v in range(HALVES):
+            flip_back(v)
+        wout_operand = quantise(wout_grouped[:].rearrange("p m k -> p (m k)"), OUT, "wout")
         nc.vector.tensor_tensor(
-            out=new_places[:, 1],
-            in0=gap[:, 1].rearrange("p e t -> p t e"),
-            in1=candidate[:, 1].rearrange("p e t -> p t e"),
+            out=new_grouped[:].rearrange("p (c i) k -> p c k i", i=LINE),
+            in0=gap[:].rearrange("p v e (c i) -> p c (v e) i", i=LINE),
+            in1=candidate[:].rearrange("p v e (c i) -> p c (v e) i", i=LINE),
             op=ADD,
         )
 
-        wout_operand = quantise(wout_grouped[:].rearrange("p m k -> p (m k)"), OUT, "wout")
         new_codes, new_scales = quantise(new_grouped[:].rearrange("p t k -> p (t k)"), TOKENS, "new")
         active = products.tile([TOKENS, OUT], F32, tag="product")
         multiply(active[:], (new_codes[:], new_scales[:]), wout_operand)

@@ -155,11 +155,11 @@ def tile_vectorizednpu_pb_s_kernel(tc, gi, registers, W_hh, b_hh, W_out, b_out, 
             w_grouped[i] = per_unit.tile([P, PAIR, P, PACK], BF16, align_bytes=64, name="w_grouped")
             nc.scalar.copy(out=w_grouped[i][:].bitcast(F32), in_=bank[:].rearrange("p (e h) m -> p e m h", h=HALVES))
 
-        def flip_half(i, e):
+        def flip_half(i, e, copy):
             if e == 0:
                 w_grouped[i] = per_unit.tile([P, PAIR, P, PACK], BF16, align_bytes=64, name="w_grouped")
             bank = flip_words(w_rows[units[i]][:, e, :].bitcast(F32))
-            nc.scalar.copy(out=w_grouped[i][:, e].bitcast(F32), in_=bank.rearrange("p h m -> p m h"))
+            copy(out=w_grouped[i][:, e].bitcast(F32), in_=bank.rearrange("p h m -> p m h"))
 
         def flip_gi(g, copy):
             gi_words = keep.tile([P, HALVES, TOKENS], F32, name="gi_words%d" % g)
@@ -226,13 +226,15 @@ def tile_vectorizednpu_pb_s_kernel(tc, gi, registers, W_hh, b_hh, W_out, b_out, 
         R0, R1, N0, N1, Z0, Z1 = range(len(units))
 
         for e in range(PAIR):
-            flip_half(R0, e)
+            flip_half(R0, e, nc.scalar.copy)
         reg_grouped = regrouped(flip_rows(regs_in), "reg")
         multiply_zeros(P // 2)
         old_state = reg_grouped[:].rearrange("p t (v e) -> p v e t", e=PAIR)
         flip_weights(R1)
         multiply_zeros(P // 2)
         quantise_weights(R0, parts=PAIR)
+        reg_operand = quantise(reg_grouped[:].rearrange("p m k -> p (m k)"), TOKENS, "reg")
+        flip_gi(GATE_R, nc.vector.tensor_copy)
         bias_bank = flipped.tile([P, BANK_SLOTS, P], F32, tag="bank")
         for c in range(BIAS_BLOCKS):
             flip(bias_bank, c, bias_rows[:, c * HALVES * P : (c + 1) * HALVES * P].bitcast(F32))
@@ -241,30 +243,28 @@ def tile_vectorizednpu_pb_s_kernel(tc, gi, registers, W_hh, b_hh, W_out, b_out, 
             out=bias[:].rearrange("p (r c) e -> p c r e", r=BIAS_ROWS),
             in_=bias_bank[:, 0:BIAS_BLOCKS, 0:BIAS_ROWS].bitcast(BF16).rearrange("p c (r e) -> p c r e", e=PAIR),
         )
-        reg_operand = quantise(reg_grouped[:].rearrange("p m k -> p (m k)"), TOKENS, "reg")
-        flip_gi(GATE_R, nc.vector.tensor_copy)
         multiply_zeros(P // 2)
         flip_weights(N0)
         quantise_weights(R1)
-        multiply_unit(R0)
-        gate_argument(R0)
         flip_weights(N1)
+        multiply_unit(R0)
         multiply_unit(R1)
+        gate_argument(R0)
         gate_argument(R1)
         quantise_weights(N0)
         flip_weights(Z0)
-        gate_function(R0)
-        flip_weights(Z1)
         quantise_weights(N1)
+        flip_half(Z1, 0, nc.scalar.copy)
+        flip_half(Z1, 1, nc.vector.tensor_copy)
+        gate_function(R0)
         gate_function(R1)
-        flip_gi(GATE_N, nc.vector.tensor_copy)
-        flip_gi(GATE_Z, nc.scalar.copy)
-        wout_flipped = flip_rows(wout_in)
+        flip_gi(GATE_N, nc.scalar.copy)
         multiply_unit(N0)
         multiply_unit(N1)
+        flip_gi(GATE_Z, nc.scalar.copy)
         quantise_weights(Z0)
+        quantise_weights(Z1, parts=PAIR)
         gate_argument(N0)
-        quantise_weights(Z1)
         gate_argument(N1)
         add_gi(N0)
         gate_function(N0)
@@ -277,7 +277,7 @@ def tile_vectorizednpu_pb_s_kernel(tc, gi, registers, W_hh, b_hh, W_out, b_out, 
         gate_function(Z0)
         gate_argument(Z1)
         gate_function(Z1)
-        wout_grouped = regrouped(wout_flipped, "wout")
+        wout_grouped = regrouped(flip_rows(wout_in), "wout")
         for v in range(HALVES):
             subtract_candidate(v)
         for v in range(HALVES):

@@ -161,9 +161,9 @@ def tile_vectorizednpu_pb_s_kernel(tc, gi, registers, W_hh, b_hh, W_out, b_out, 
             bank = flip_words(w_rows[units[i]][:, e, :].bitcast(F32))
             copy(out=w_grouped[i][:, e].bitcast(F32), in_=bank.rearrange("p h m -> p m h"))
 
-        def flip_gi(g, copy):
+        def flip_gi(g):
             gi_words = keep.tile([P, HALVES, TOKENS], F32, name="gi_words%d" % g)
-            copy(out=gi_words[:], in_=flip_rows(gi_in[g]))
+            nc.scalar.copy(out=gi_words[:], in_=flip_rows(gi_in[g]))
             gi_values[g] = gi_words[:].bitcast(BF16).rearrange("p v (t e) -> p v e t", e=PAIR)
 
         def quantise_weights(i, parts=1):
@@ -234,7 +234,7 @@ def tile_vectorizednpu_pb_s_kernel(tc, gi, registers, W_hh, b_hh, W_out, b_out, 
         multiply_zeros(P // 2)
         quantise_weights(R0, parts=PAIR)
         reg_operand = quantise(reg_grouped[:].rearrange("p m k -> p (m k)"), TOKENS, "reg")
-        flip_gi(GATE_R, nc.vector.tensor_copy)
+        flip_gi(GATE_R)
         bias_bank = flipped.tile([P, BANK_SLOTS, P], F32, tag="bank")
         for c in range(BIAS_BLOCKS):
             flip(bias_bank, c, bias_rows[:, c * HALVES * P : (c + 1) * HALVES * P].bitcast(F32))
@@ -246,8 +246,9 @@ def tile_vectorizednpu_pb_s_kernel(tc, gi, registers, W_hh, b_hh, W_out, b_out, 
         multiply_zeros(P // 2)
         flip_weights(N0)
         quantise_weights(R1)
-        flip_weights(N1)
+        multiply_zeros(P // 2)
         multiply_unit(R0)
+        flip_weights(N1)
         multiply_unit(R1)
         gate_argument(R0)
         gate_argument(R1)
@@ -258,10 +259,11 @@ def tile_vectorizednpu_pb_s_kernel(tc, gi, registers, W_hh, b_hh, W_out, b_out, 
         flip_half(Z1, 1, nc.vector.tensor_copy)
         gate_function(R0)
         gate_function(R1)
-        flip_gi(GATE_N, nc.scalar.copy)
+        flip_gi(GATE_N)
         multiply_unit(N0)
         multiply_unit(N1)
-        flip_gi(GATE_Z, nc.scalar.copy)
+        flip_gi(GATE_Z)
+        multiply_codes(N1, 4)
         quantise_weights(Z0)
         quantise_weights(Z1, parts=PAIR)
         gate_argument(N0)

from contextlib import ExitStack

import concourse.mybir as mybir
from concourse.masks import make_identity

F32 = mybir.dt.float32
BF16 = mybir.dt.bfloat16
U32 = mybir.dt.uint32
U8 = mybir.dt.uint8
FP8X4 = mybir.dt.float8_e4m3fn_x4
ADD = mybir.AluOpType.add
SUBTRACT = mybir.AluOpType.subtract
MULT = mybir.AluOpType.mult
SIGMOID = mybir.ActivationFunctionType.Sigmoid
TANH = mybir.ActivationFunctionType.Tanh

P = 128
TOKENS = 128
STATE = 512
OUT = 128
HALVES = 2
PAIR = 2
PACK = HALVES * PAIR
GATES = 3
GATE_R, GATE_Z, GATE_N = 0, 1, 2
GATE_ORDER = (GATE_R, GATE_N, GATE_Z)
BIAS_ROWS = 2
BIAS_BLOCKS = GATES * HALVES // BIAS_ROWS
LINE = 4
BANK_SLOTS = 4

FLOPS = 2 * TOKENS * STATE * (GATES * STATE + OUT)


def tile_vectorizednpu_pb_s_kernel(tc, gi, registers, W_hh, b_hh, W_out, b_out, out_0, out_1):
    nc = tc.nc
    units = [(g, v) for g in GATE_ORDER for v in range(HALVES)]
    with ExitStack() as ctx:
        ctx.enter_context(tc.manual_schedule())
        keep = ctx.enter_context(tc.tile_pool(name="keep", bufs=1))
        per_unit = ctx.enter_context(tc.tile_pool(name="per_unit", bufs=GATES * HALVES))
        flipped = ctx.enter_context(tc.psum_pool(name="flipped", bufs=5))
        products = ctx.enter_context(tc.psum_pool(name="products", bufs=2))
        unread = ctx.enter_context(tc.psum_pool(name="unread", bufs=1))

        identity = keep.tile([P, P], F32)
        make_identity(nc, identity[:])

        zeros = keep.tile([P, P], F32)
        nc.vector.memset(zeros[:], 0.0)

        regs_in = keep.tile([TOKENS, STATE], BF16)
        bias_rows = keep.tile([P, BIAS_BLOCKS * HALVES * P], BF16)
        nc.vector.memset(bias_rows[:], 0.0)
        w_view = W_hh.rearrange("(g v p e) k -> g v p e k", g=GATES, v=HALVES, p=P, e=PAIR)
        gi_flat = gi.flatten_outer_dims()
        gi_in = {}

        def load_gi(g):
            nc.sync.dma_start(out=gi_in[g][:], in_=gi_flat[:, g * STATE : (g + 1) * STATE])

        w_rows = {}
        for g in GATE_ORDER:
            for v in range(HALVES):
                w_rows[(g, v)] = per_unit.tile([P, PAIR, STATE], BF16, name="w_rows")
                if (g, v) == units[0]:
                    for e in range(PAIR):
                        nc.sync.dma_start(out=w_rows[(g, v)][:, e, :], in_=w_view[g, v, :, e, :])
                else:
                    nc.sync.dma_start(out=w_rows[(g, v)][:], in_=w_view[g, v])
                if (g, v) == units[0]:
                    nc.sync.dma_start(out=regs_in[:], in_=registers.flatten_outer_dims())
                if (g, v) == units[1]:
                    nc.sync.dma_start(out=bias_rows[0:BIAS_ROWS, :], in_=b_hh.rearrange("(r c) -> r c", r=BIAS_ROWS))
            gi_in[g] = keep.tile([TOKENS, STATE], BF16, name="gi_in%d" % g)
            if g == GATE_R:
                load_gi(g)
        for g in (GATE_N, GATE_Z):
            load_gi(g)
        wout_in = keep.tile([OUT, STATE], BF16)
        nc.sync.dma_start(out=wout_in[:], in_=W_out)
        bout_all = keep.tile([P, OUT], BF16)
        nc.sync.dma_start(out=bout_all[:], in_=b_out.partition_broadcast(P))

        table = keep.tile([P, 1], F32)
        nc.scalar.activation(out=table[:], in_=zeros[:, 0:1], func=SIGMOID)
        idle = unread.tile([P, PAIR * P], F32)

        def multiply_zeros(columns):
            nc.tensor.matmul(out=idle[:, 0:columns], lhsT=zeros[:], rhs=zeros[:, 0:columns], start=True, stop=True)

        for n in range(3):
            multiply_zeros(P)

        def flip(bank, slot, words):
            nc.tensor.transpose(out=bank[:, slot, :], in_=words, identity=identity[:])

        def flip_rows(rows_in):
            return flip_words(rows_in[:].bitcast(F32))

        def flip_words(words):
            bank = flipped.tile([P, BANK_SLOTS, P], F32, tag="bank")
            for v in range(HALVES):
                flip(bank, v, words[:, v * P : (v + 1) * P])
            return bank[:, 0:HALVES, :]

        def quantise(grouped, width, name, parts=1):
            codes = per_unit.tile([P, width], U32, align_bytes=64, name=name + "_codes")
            scales = per_unit.tile([P, width], U8, align_bytes=64, name=name + "_scales")
            part = width // parts
            for first in range(0, width, part):
                columns = slice(first, first + part)
                nc.vector.quantize_mx(
                    out=codes[:, columns].bitcast(FP8X4),
                    scales=scales[:, columns],
                    in_=grouped[:, first * PACK : (first + part) * PACK],
                )
            return codes, scales

        def regrouped(flipped_rows, name):
            grouped = keep.tile([P, P, PACK], BF16, align_bytes=64, name=name + "_grouped")
            nc.scalar.copy(out=grouped[:].bitcast(F32), in_=flipped_rows.rearrange("p v m -> p m v"))
            return grouped

        def multiply(out, stationary, moving):
            nc.tensor.matmul_mx(
                out=out,
                lhsT=stationary[0].bitcast(FP8X4),
                lhsT_scale=stationary[1],
                rhs=moving[0][:].bitcast(FP8X4),
                rhs_scale=moving[1][:],
                start=True,
                stop=True,
            )

        gi_values = {}
        w_grouped = {}
        w_operand = {}
        gh = {}
        gate_arg = {}
        back = {}
        reset = keep.tile([P, HALVES, PAIR, TOKENS], F32)
        candidate = keep.tile([P, HALVES, PAIR, TOKENS], F32)
        update = keep.tile([P, HALVES, PAIR, TOKENS], F32)
        gate_value = {GATE_R: reset, GATE_N: candidate, GATE_Z: update}
        gap = keep.tile([P, HALVES, PAIR, TOKENS], F32)
        new_grouped = keep.tile([P, TOKENS, PACK], BF16, align_bytes=64)

        def flip_weights(i):
            words = w_rows[units[i]][:].bitcast(F32)
            bank = flipped.tile([P, BANK_SLOTS, P], F32, tag="bank")
            for e in range(PAIR):
                for k_half in range(HALVES):
                    flip(bank, HALVES * e + k_half, words[:, e, k_half * P : (k_half + 1) * P])
            w_grouped[i] = per_unit.tile([P, PAIR, P, PACK], BF16, align_bytes=64, name="w_grouped")
            nc.scalar.copy(out=w_grouped[i][:].bitcast(F32), in_=bank[:].rearrange("p (e h) m -> p e m h", h=HALVES))

        def flip_half(i, e, copy):
            if e == 0:
                w_grouped[i] = per_unit.tile([P, PAIR, P, PACK], BF16, align_bytes=64, name="w_grouped")
            bank = flip_words(w_rows[units[i]][:, e, :].bitcast(F32))
            copy(out=w_grouped[i][:, e].bitcast(F32), in_=bank.rearrange("p h m -> p m h"))

        def flip_gi(g):
            gi_words = keep.tile([P, HALVES, TOKENS], F32, name="gi_words%d" % g)
            nc.scalar.copy(out=gi_words[:], in_=flip_rows(gi_in[g]))
            gi_values[g] = gi_words[:].bitcast(BF16).rearrange("p v (t e) -> p v e t", e=PAIR)

        def quantise_weights(i, parts=1):
            grouped = w_grouped[i][:].rearrange("p e m k -> p (e m k)")
            w_operand[i] = quantise(grouped, PAIR * P, "w", parts)

        def multiply_codes(i, times):
            w_codes, w_scales = w_operand[i]
            for n in range(times):
                multiply(idle[:], (w_codes[:, 0:P], w_scales[:, 0:P]), (w_codes, w_scales))

        def multiply_unit(i):
            w_codes, w_scales = w_operand[i]
            gh[i] = products.tile([P, PAIR, TOKENS], F32, tag="product", name="gh")
            for e in range(PAIR):
                rows = slice(e * P, (e + 1) * P)
                multiply(gh[i][:, e, :], (w_codes[:, rows], w_scales[:, rows]), reg_operand)

        def gate_argument(i):
            g, v = units[i]
            other, op = (reset[:, v], MULT) if g == GATE_N else (gi_values[g][:, v], ADD)
            gate_arg[i] = per_unit.tile([P, PAIR, TOKENS], F32, name="gate_arg")
            for e in range(PAIR):
                nc.vector.scalar_tensor_tensor(
                    out=gate_arg[i][:, e, :],
                    in0=gh[i][:, e, :],
                    scalar=bias[:, HALVES * g + v, e : e + 1],
                    in1=other[:, e, :],
                    op0=ADD,
                    op1=op,
                )

        def add_gi(i):
            g, v = units[i]
            nc.vector.tensor_tensor(out=gate_arg[i][:], in0=gate_arg[i][:], in1=gi_values[g][:, v], op=ADD)

        def gate_function(i):
            g, v = units[i]
            nc.scalar.activation(out=gate_value[g][:, v], in_=gate_arg[i][:], func=TANH if g == GATE_N else SIGMOID)

        def subtract_candidate(v):
            nc.vector.tensor_tensor(out=gap[:, v], in0=old_state[:, v], in1=candidate[:, v], op=SUBTRACT)

        def scale_gap(v):
            nc.vector.tensor_tensor(out=gap[:, v], in0=update[:, v], in1=gap[:, v], op=MULT)

        def flip_back(v):
            back[v] = flipped.tile([TOKENS, BANK_SLOTS, P], F32, tag="bank", name="back")
            for e in range(PAIR):
                for term, first in ((candidate, True), (gap, False)):
                    nc.tensor.matmul(
                        out=back[v][:, e, :],
                        lhsT=term[:, v, e, :],
                        rhs=identity[:],
                        is_transpose=True,
                        start=first,
                        stop=not first,
                    )

        R0, R1, N0, N1, Z0, Z1 = range(len(units))

        for e in range(PAIR):
            flip_half(R0, e, nc.scalar.copy)
        reg_grouped = regrouped(flip_rows(regs_in), "reg")
        multiply_zeros(P // 2)
        old_state = reg_grouped[:].rearrange("p t (v e) -> p v e t", e=PAIR)
        flip_weights(R1)
        multiply_zeros(P // 2)
        quantise_weights(R0, parts=PAIR)
        reg_operand = quantise(reg_grouped[:].rearrange("p m k -> p (m k)"), TOKENS, "reg")
        flip_gi(GATE_R)
        bias_bank = flipped.tile([P, BANK_SLOTS, P], F32, tag="bank")
        for c in range(BIAS_BLOCKS):
            flip(bias_bank, c, bias_rows[:, c * HALVES * P : (c + 1) * HALVES * P].bitcast(F32))
        bias = keep.tile([P, GATES * HALVES, PAIR], F32)
        nc.vector.tensor_copy(
            out=bias[:].rearrange("p (r c) e -> p c r e", r=BIAS_ROWS),
            in_=bias_bank[:, 0:BIAS_BLOCKS, 0:BIAS_ROWS].bitcast(BF16).rearrange("p c (r e) -> p c r e", e=PAIR),
        )
        multiply_zeros(P // 2)
        flip_weights(N0)
        quantise_weights(R1)
        multiply_zeros(P // 2)
        multiply_unit(R0)
        flip_weights(N1)
        multiply_unit(R1)
        gate_argument(R0)
        gate_argument(R1)
        quantise_weights(N0)
        flip_weights(Z0)
        quantise_weights(N1)
        flip_half(Z1, 0, nc.scalar.copy)
        flip_half(Z1, 1, nc.vector.tensor_copy)
        gate_function(R0)
        gate_function(R1)
        flip_gi(GATE_N)
        multiply_unit(N0)
        multiply_unit(N1)
        flip_gi(GATE_Z)
        multiply_codes(N1, 4)
        quantise_weights(Z0)
        quantise_weights(Z1, parts=PAIR)
        gate_argument(N0)
        gate_argument(N1)
        add_gi(N0)
        gate_function(N0)
        add_gi(N1)
        gate_function(N1)
        multiply_unit(Z0)
        multiply_unit(Z1)
        multiply_codes(Z1, 6)
        gate_argument(Z0)
        gate_function(Z0)
        gate_argument(Z1)
        gate_function(Z1)
        wout_grouped = regrouped(flip_rows(wout_in), "wout")
        for v in range(HALVES):
            subtract_candidate(v)
        for v in range(HALVES):
            scale_gap(v)

        for v in range(HALVES):
            flip_back(v)
        wout_operand = quantise(wout_grouped[:].rearrange("p m k -> p (m k)"), OUT, "wout")
        nc.vector.tensor_tensor(
            out=new_grouped[:].rearrange("p (c i) k -> p c k i", i=LINE),
            in0=gap[:].rearrange("p v e (c i) -> p c (v e) i", i=LINE),
            in1=candidate[:].rearrange("p v e (c i) -> p c (v e) i", i=LINE),
            op=ADD,
        )

        new_codes, new_scales = quantise(new_grouped[:].rearrange("p t k -> p (t k)"), TOKENS, "new")
        active = products.tile([TOKENS, OUT], F32, tag="product")
        multiply(active[:], (new_codes[:], new_scales[:]), wout_operand)

        out_1_flat = out_1.flatten_outer_dims()
        for v in range(HALVES):
            new_out = per_unit.tile([TOKENS, P, PAIR], F32, name="new_out")
            nc.scalar.copy(out=new_out[:], in_=back[v][:, 0:PAIR, :].rearrange("t e p -> t p e"))
            queue = (nc.sync, nc.scalar)[v]
            queue.dma_start(
                out=out_1_flat[:, v * PAIR * P : (v + 1) * PAIR * P], in_=new_out[:].rearrange("t p e -> t (p e)")
            )

        active_out = keep.tile([TOKENS, OUT], F32)
        nc.vector.tensor_tensor(out=active_out[:], in0=active[:], in1=bout_all[:], op=ADD)
        nc.sync.dma_start(out=out_0.flatten_outer_dims(), in_=active_out[:])
